import numpy as np
import ml_dtypes


def mxq(x, axis, fmt="e4m3"):
    dtype, down = {"e4m3": (ml_dtypes.float8_e4m3fn, 7), "e5m2": (ml_dtypes.float8_e5m2, 14)}[fmt]
    v = np.moveaxis(np.asarray(x, np.float32).astype(ml_dtypes.bfloat16).astype(np.float64), axis, -1)
    blocks = v.reshape(v.shape[:-1] + (-1, 32))
    amax = np.abs(blocks).max(-1, keepdims=True)
    byte = np.maximum(np.where(amax > 0, np.frexp(amax)[1] - 1 + 127, 0) - down, 1)
    scale = np.exp2(byte - 127.0)
    codes = (blocks / scale).astype(np.float32).astype(dtype).astype(np.float64)
    return np.moveaxis((codes * scale).reshape(v.shape), -1, axis)


WIDE = False


def mx_kscale(k):
    if not WIDE:
        return np.ones(k)
    levels = np.array([10, -10, 5, -5, 0])
    if k % 512:
        return np.exp2(np.random.permutation(np.resize(levels, k // 32))).repeat(32)
    a = np.empty((k // 512, 16))
    for p in range(k // 512):
        a[p, :8] = np.random.permutation(np.resize(levels, 8))
        for g in range(8):
            far = levels[np.abs(levels - a[p, g]) >= 10]
            a[p, g + 8] = far[np.random.randint(len(far))]
    return np.exp2(a.ravel()).repeat(32)


BF16 = ml_dtypes.bfloat16


def bf(x):
    return np.asarray(x, np.float32).astype(BF16)


def f64(x):
    return np.asarray(x).astype(np.float64)


B, T, P, F, G, R, C, O = 256, 8, 1024, 512, 512, 128, 4, 10


def setup_inputs():
    s, t = mx_kscale(P + F), mx_kscale(G)
    u = np.roll(t, R)
    r0 = np.concatenate([1.0 / (np.sqrt(P + F) * s), [0.1]])[:, None]
    r1 = np.concatenate([1.5 / (np.sqrt(G) * t), [0.1]])[:, None]
    return {"primary_input": bf((np.random.standard_normal((B, T, P)) * s[:P]).reshape(B, T * P)),
            "prev": bf((np.maximum(np.random.standard_normal((B, T, F)), 0.0) * 0.9 * s[P:]).reshape(B, T * F)),
            "col": bf(np.array([float(np.random.randint(1, C))])),
            "W0": bf(np.random.standard_normal((P + F + 1, G)) * r0 * u),
            "b0": bf(np.random.standard_normal(G) * 0.2 * u),
            "W1": bf(np.random.standard_normal((G + 1, F)) * r1),
            "b1": bf(np.random.standard_normal(F) * 0.2)}


def reference(primary_input, prev, col, W0, b0, W1, b1):
    w0, w1, c = f64(W0), f64(W1), f64(col)
    inp = np.concatenate([f64(primary_input).reshape(B, T, P), f64(prev).reshape(B, T, F)], axis=-1)
    a = (mxq(inp, 2, "e4m3") @ mxq(w0[:P + F], 0, "e4m3")) + c * w0[P + F] + f64(b0)
    h = np.roll(np.maximum(a, 0.0).reshape(B, T * G), -R, axis=1).reshape(B, T, G)
    y = (mxq(h, 2, "e4m3") @ mxq(w1[:G], 0, "e4m3")) + c * w1[G] + f64(b1)
    return np.roll(np.maximum(y, 0.0).reshape(B, T * F), R, axis=1)

@@ -1,0 +1,244 @@
+from contextlib import ExitStack
+
+import concourse.mybir as mybir
+from concourse.masks import make_identity
+
+F32 = mybir.dt.float32
+BF16 = mybir.dt.bfloat16
+U32 = mybir.dt.uint32
+U8 = mybir.dt.uint8
+FP8X4 = mybir.dt.float8_e4m3fn_x4
+RELU = mybir.ActivationFunctionType.Relu
+ADD = mybir.AluOpType.add
+
+FLOPS = 2 * 2048 * (1536 * 512 + 512 * 512)
+
+UNITS = 8
+PASSES = 3
+
+AHEAD_X = 2
+LAG_G = 1
+LAG_H = 2
+LAG_OUT = 3
+
+
+def tile_capsuleneuralnetwork_pa_kernel(tc, primary_input, prev, col, W0, b0, W1, b1, out):
+    nc = tc.nc
+    with ExitStack() as ctx:
+        keep = ctx.enter_context(tc.tile_pool(name="keep", bufs=1))
+        stage = ctx.enter_context(tc.tile_pool(name="stage", bufs=6))
+        ps_t = ctx.enter_context(tc.psum_pool(name="ps_t", bufs=3))
+        ps_a = ctx.enter_context(tc.psum_pool(name="ps_a", bufs=3))
+        ps_y = ctx.enter_context(tc.psum_pool(name="ps_y", bufs=2))
+        ctx.enter_context(tc.manual_schedule())
+
+        ident = keep.tile([128, 128], F32, name="ident")
+        make_identity(nc, ident[:])
+        bias_rows = keep.tile([128, 1024], BF16, name="bias_rows")
+        nc.vector.memset(bias_rows[:], 0.0)
+        col_ones = keep.tile([128, 128], BF16, name="col_ones")
+        nc.gpsimd.memset(col_ones[:], 0.0)
+        nc.gpsimd.memset(col_ones[32:64, :], 1.0)
+        col_sb = keep.tile([1, 1], BF16, name="col_sb")
+        nc.scalar.dma_start(out=col_sb[0:1, 0:1], in_=col.unsqueeze(0))
+        nc.gpsimd.tensor_copy(out=col_ones[0:1, :], in_=col_sb[0:1, 0:1].to_broadcast([1, 128]))
+        nc.scalar.dma_start(out=bias_rows[0:1, 0:384], in_=W0[1536:1537, 128:512])
+        nc.scalar.dma_start(out=bias_rows[0:1, 384:512], in_=W0[1536:1537, 0:128])
+        nc.scalar.dma_start(out=bias_rows[32:33, 0:384], in_=b0[128:512].unsqueeze(0))
+        nc.scalar.dma_start(out=bias_rows[32:33, 384:512], in_=b0[0:128].unsqueeze(0))
+        nc.scalar.dma_start(out=bias_rows[0:1, 512:1024], in_=W1[512:513, :])
+        nc.scalar.dma_start(out=bias_rows[32:33, 512:1024], in_=b1.unsqueeze(0))
+
+        prim = [keep.tile([128, 2, 1024], BF16, name="prim%d" % u) for u in range(UNITS)]
+        prv = [keep.tile([128, 2, 512], BF16, name="prv%d" % u) for u in range(UNITS)]
+        w_raw = [keep.tile([128, 4, 512], BF16, name="w_raw%d" % g) for g in range(4)]
+
+        def load_primary(t):
+            nc.sync.dma_start(out=prim[t][:],
+                              in_=primary_input[:, 1024 * t:1024 * t + 1024].rearrange("(h p) k -> p h k", h=2))
+
+        def load_prev(t):
+            nc.sync.dma_start(out=prv[t][:],
+                              in_=prev[:, 512 * t:512 * t + 512].rearrange("(h p) k -> p h k", h=2))
+
+        def load_w0(g):
+            nc.sync.dma_start(out=w_raw[g][:], in_=W0[512 * g:512 * g + 512, :].rearrange("(p j) c -> p j c", j=4))
+
+        def load_w1():
+            nc.sync.dma_start(out=w_raw[3][:], in_=W1[0:512, :].rearrange("(p j) n -> p j n", j=4))
+
+        load_primary(0)
+        load_w0(0)
+        load_prev(0)
+        load_w0(1)
+        load_w0(2)
+        for t in (1, 2):
+            load_primary(t)
+            load_prev(t)
+        load_w1()
+        for t in range(3, UNITS):
+            load_primary(t)
+            load_prev(t)
+
+        w_g = [keep.tile([128, 2048], BF16, name="w_g%d" % g, align_bytes=64) for g in range(4)]
+        w_c = [keep.tile([128, 512], U32, name="w_c%d" % g, align_bytes=64) for g in range(4)]
+        w_s = [keep.tile([128, 512], U8, name="w_s%d" % g, align_bytes=64) for g in range(4)]
+        x_c = [keep.tile([128, PASSES, 256], U32, name="x_c%d" % t, align_bytes=64) for t in range(UNITS)]
+        x_s = [keep.tile([128, PASSES, 256], U8, name="x_s%d" % t, align_bytes=64) for t in range(UNITS)]
+        h_t = [keep.tile([128, 4, 256], BF16, name="h_t%d" % t) for t in range(UNITS)]
+        h_g = [keep.tile([128, 1024], BF16, name="h_g%d" % t, align_bytes=64) for t in range(UNITS)]
+        h_c = [keep.tile([128, 256], U32, name="h_c%d" % t, align_bytes=64) for t in range(UNITS)]
+        h_s = [keep.tile([128, 256], U8, name="h_s%d" % t, align_bytes=64) for t in range(UNITS)]
+        o_sb = [keep.tile([128, 2, 512], F32, name="o_sb%d" % t) for t in range(UNITS)]
+        bias0 = keep.tile([128, 4], F32, name="bias0")
+        bias1 = keep.tile([128, 512], F32, name="bias1")
+
+        def regroup(dst, src):
+            nc.vector.tensor_copy(
+                out=dst.rearrange("p (c i t) -> p c t i", i=4, t=4),
+                in_=src.rearrange("p t (c i) -> p c t i", i=4),
+            )
+
+        def quantise(codes, scales, src):
+            nc.vector.quantize_mx(out=codes.bitcast(FP8X4), scales=scales, in_=src)
+
+        banks = {}
+        x_g = {}
+
+        def transpose_inputs(t):
+            for g in range(PASSES):
+                words = (prim[t] if g < 2 else prv[t])[:].bitcast(F32)
+                base = 256 * g if g < 2 else 0
+                bank = ps_t.tile([128, 2, 2, 128], F32, name="bank", tag="tp")
+                banks[(t, g)] = bank
+                for half in range(2):
+                    for e in range(2):
+                        nc.tensor.transpose(bank[:, half, e, :], words[:, half, base + e:base + 256:2], ident[:])
+
+        def copy_inputs(t):
+            for g in range(PASSES):
+                grp = stage.tile([128, 1024], BF16, name="x_g", tag="x_g", align_bytes=64)
+                x_g[(t, g)] = grp
+                dst = grp[:].bitcast(F32).rearrange("p (t b h) -> p t b h", t=2, b=128, h=2)
+                src = banks[(t, g)][:].rearrange("p t h b -> p t b h")
+                if g == 2 and t >= 3:
+                    nc.vector.tensor_copy(out=dst, in_=src)
+                else:
+                    nc.scalar.copy(out=dst, in_=src)
+
+        def quantise_inputs(t):
+            for g in range(PASSES):
+                quantise(x_c[t][:, g, :], x_s[t][:, g, :], x_g[(t, g)][:])
+
+        def regroup_weights(g):
+            if g == 3:
+                regroup(w_g[g][:], w_raw[g][:])
+                return
+            dst = w_g[g][:].rearrange("p (t m j) -> p t m j", t=4, j=4)
+            src = w_raw[g][:].rearrange("p j (m t) -> p t m j", t=4)
+            nc.vector.tensor_copy(out=dst[:, :, 0:96, :], in_=src[:, :, 32:128, :])
+            nc.vector.tensor_copy(out=dst[:, :, 96:128, :], in_=src[:, :, 0:32, :])
+
+        def quantise_weights(g):
+            quantise(w_c[g][:], w_s[g][:], w_g[g][:])
+
+        def biases():
+            pb0 = ps_y.tile([128, 4, 64], F32, name="pb0", tag="y")
+            for j in range(4):
+                nc.tensor.matmul(out=pb0[:, j, :], lhsT=bias_rows[:, j:512:4], rhs=col_ones[:, 0:64],
+                                 start=True, stop=True)
+            nc.scalar.copy(out=bias0[:], in_=pb0[:, :, 0])
+            pb1 = ps_y.tile([128, 512], F32, name="pb1", tag="y")
+            nc.tensor.matmul(out=pb1[:], lhsT=col_ones[:], rhs=bias_rows[:, 512:1024], start=True, stop=True)
+            nc.scalar.copy(out=bias1[:], in_=pb1[:])
+
+        def layer1(t):
+            for pair in range(2):
+                acc = ps_a.tile([128, 2, 256], F32, name="acc", tag="acc")
+                for i in range(2):
+                    j = 2 * pair + i
+                    for g in range(PASSES):
+                        nc.tensor.matmul_mx(
+                            out=acc[:, i, :],
+                            lhsT=w_c[g][:, 128 * j:128 * j + 128].bitcast(FP8X4),
+                            lhsT_scale=w_s[g][:, 128 * j:128 * j + 128],
+                            rhs=x_c[t][:, g, :].bitcast(FP8X4),
+                            rhs_scale=x_s[t][:, g, :],
+                            start=(g == 0),
+                            stop=(g == PASSES - 1),
+                        )
+                for i in range(2):
+                    j = 2 * pair + i
+                    nc.scalar.activation(out=h_t[t][:, j, :], in_=acc[:, i, :], func=RELU,
+                                         bias=bias0[:, j:j + 1], scale=1.0)
+
+        def regroup_h(t):
+            before = (t - 1) % UNITS
+            regroup(h_g[before][96:128, :], h_t[t][96:128])
+            regroup(h_g[t][0:96, :], h_t[t][0:96])
+
+        def quantise_h(t):
+            quantise(h_c[t][:], h_s[t][:], h_g[t][:])
+
+        def layer2(t):
+            ys = []
+            for half in range(2):
+                y = ps_y.tile([128, 512], F32, name="y", tag="y")
+                ys.append(y)
+                nc.tensor.matmul_mx(
+                    out=y[:],
+                    lhsT=h_c[t][:, 128 * half:128 * half + 128].bitcast(FP8X4),
+                    lhsT_scale=h_s[t][:, 128 * half:128 * half + 128],
+                    rhs=w_c[3][:].bitcast(FP8X4),
+                    rhs_scale=w_s[3][:],
+                    start=True,
+                    stop=True,
+                )
+            for half in range(2):
+                nc.vector.tensor_tensor(out=o_sb[t][:, half, :], in0=ys[half][:], in1=bias1[:], op=ADD)
+
+        def finish(t):
+            for half in range(2):
+                piece = o_sb[t][:, half, :]
+                nc.scalar.activation(out=piece, in_=piece, func=RELU)
+                rows = out[128 * half:128 * half + 128, :]
+                if t < UNITS - 1:
+                    nc.sync.dma_start(out=rows[:, 512 * t + 128:512 * t + 640], in_=piece)
+                else:
+                    nc.sync.dma_start(out=rows[:, 3712:4096], in_=o_sb[t][:, half, 0:384])
+                    nc.sync.dma_start(out=rows[:, 0:128], in_=o_sb[t][:, half, 384:512])
+
+        transpose_inputs(0)
+        copy_inputs(0)
+        biases()
+        regroup_weights(0)
+        regroup_weights(1)
+        quantise_weights(0)
+        quantise_inputs(0)
+        regroup_weights(2)
+        quantise_weights(1)
+        quantise_weights(2)
+        transpose_inputs(1)
+        copy_inputs(1)
+        quantise_inputs(1)
+
+        for s in range(UNITS + LAG_OUT):
+            if s + AHEAD_X < UNITS:
+                transpose_inputs(s + AHEAD_X)
+                copy_inputs(s + AHEAD_X)
+            if s < UNITS:
+                layer1(s)
+            if 0 <= s - LAG_G < UNITS:
+                regroup_h(s - LAG_G)
+            if s == 0:
+                regroup_weights(3)
+            if 0 <= s - LAG_H < UNITS:
+                quantise_h(s - LAG_H)
+            if s + AHEAD_X < UNITS:
+                quantise_inputs(s + AHEAD_X)
+            if s == 0:
+                quantise_weights(3)
+            if 0 <= s - LAG_H < UNITS:
+                layer2(s - LAG_H)
+            if 0 <= s - LAG_OUT < UNITS:
+                finish(s - LAG_OUT)

@@ -16,11 +16,6 @@ FLOPS = 2 * 2048 * (1536 * 512 + 512 * 512)
 UNITS = 8
 PASSES = 3
 
-AHEAD_X = 2
-LAG_G = 1
-LAG_H = 2
-LAG_OUT = 3
-
 
 def tile_capsuleneuralnetwork_pa_kernel(tc, primary_input, prev, col, W0, b0, W1, b1, out):
     nc = tc.nc
@@ -31,6 +26,10 @@ def tile_capsuleneuralnetwork_pa_kernel(tc, primary_input, prev, col, W0, b0, W1
         ps_a = ctx.enter_context(tc.psum_pool(name="ps_a", bufs=3))
         ps_y = ctx.enter_context(tc.psum_pool(name="ps_y", bufs=2))
         ctx.enter_context(tc.manual_schedule())
+
+        warm = keep.tile([128, 1], F32, name="warm")
+        nc.gpsimd.memset(warm[:], 0.0)
+        nc.scalar.activation(out=warm[:], in_=warm[:], func=RELU)
 
         ident = keep.tile([128, 128], F32, name="ident")
         make_identity(nc, ident[:])
@@ -104,6 +103,8 @@ def tile_capsuleneuralnetwork_pa_kernel(tc, primary_input, prev, col, W0, b0, W1
 
         banks = {}
         x_g = {}
+        accs = {}
+        ys = {}
 
         def transpose_inputs(t):
             for g in range(PASSES):
@@ -121,13 +122,10 @@ def tile_capsuleneuralnetwork_pa_kernel(tc, primary_input, prev, col, W0, b0, W1
                 x_g[(t, g)] = grp
                 dst = grp[:].bitcast(F32).rearrange("p (t b h) -> p t b h", t=2, b=128, h=2)
                 src = banks[(t, g)][:].rearrange("p t h b -> p t b h")
-                if g == 2 and t >= 3:
-                    nc.vector.tensor_copy(out=dst, in_=src)
-                else:
-                    nc.scalar.copy(out=dst, in_=src)
+                nc.scalar.copy(out=dst, in_=src)
 
-        def quantise_inputs(t):
-            for g in range(PASSES):
+        def quantise_inputs(t, passes=range(PASSES)):
+            for g in passes:
                 quantise(x_c[t][:, g, :], x_s[t][:, g, :], x_g[(t, g)][:])
 
         def regroup_weights(g):
@@ -155,6 +153,7 @@ def tile_capsuleneuralnetwork_pa_kernel(tc, primary_input, prev, col, W0, b0, W1
         def layer1(t):
             for pair in range(2):
                 acc = ps_a.tile([128, 2, 256], F32, name="acc", tag="acc")
+                accs[(t, pair)] = acc
                 for i in range(2):
                     j = 2 * pair + i
                     for g in range(PASSES):
@@ -167,24 +166,37 @@ def tile_capsuleneuralnetwork_pa_kernel(tc, primary_input, prev, col, W0, b0, W1
                             start=(g == 0),
                             stop=(g == PASSES - 1),
                         )
-                for i in range(2):
-                    j = 2 * pair + i
-                    nc.scalar.activation(out=h_t[t][:, j, :], in_=acc[:, i, :], func=RELU,
-                                         bias=bias0[:, j:j + 1], scale=1.0)
+
+        def relu_h(t):
+            for j in range(4):
+                nc.scalar.activation(out=h_t[t][:, j, :], in_=accs[(t, j // 2)][:, j % 2, :], func=RELU,
+                                     bias=bias0[:, j:j + 1], scale=1.0)
 
         def regroup_h(t):
-            before = (t - 1) % UNITS
-            regroup(h_g[before][96:128, :], h_t[t][96:128])
-            regroup(h_g[t][0:96, :], h_t[t][0:96])
+            regroup(h_g[t][:], h_t[t][:])
+
+        def roll_h(t):
+            nc.vector.tensor_copy(out=h_g[(t - 1) % UNITS][96:128, :], in_=h_g[t][96:128, :])
+
+        def regroup_and_roll_last_h():
+            regroup(h_g[UNITS - 2][96:128, :], h_t[UNITS - 1][96:128])
+            regroup(h_g[UNITS - 1][0:96, :], h_t[UNITS - 1][0:96])
 
         def quantise_h(t):
             quantise(h_c[t][:], h_s[t][:], h_g[t][:])
 
+        def store(t, half):
+            rows = out[128 * half:128 * half + 128, :]
+            if t < UNITS - 1:
+                nc.sync.dma_start(out=rows[:, 512 * t + 128:512 * t + 640], in_=o_sb[t][:, half, :])
+            else:
+                nc.sync.dma_start(out=rows[:, 3712:4096], in_=o_sb[t][:, half, 0:384])
+                nc.sync.dma_start(out=rows[:, 0:128], in_=o_sb[t][:, half, 384:512])
+
         def layer2(t):
-            ys = []
             for half in range(2):
                 y = ps_y.tile([128, 512], F32, name="y", tag="y")
-                ys.append(y)
+                ys[(t, half)] = y
                 nc.tensor.matmul_mx(
                     out=y[:],
                     lhsT=h_c[t][:, 128 * half:128 * half + 128].bitcast(FP8X4),
@@ -194,19 +206,17 @@ def tile_capsuleneuralnetwork_pa_kernel(tc, primary_input, prev, col, W0, b0, W1
                     start=True,
                     stop=True,
                 )
-            for half in range(2):
-                nc.vector.tensor_tensor(out=o_sb[t][:, half, :], in0=ys[half][:], in1=bias1[:], op=ADD)
 
-        def finish(t):
-            for half in range(2):
-                piece = o_sb[t][:, half, :]
+        def add_bias(t, half):
+            nc.vector.tensor_tensor(out=o_sb[t][:, half, :], in0=ys[(t, half)][:], in1=bias1[:], op=ADD)
+
+        def finish(t, half, engine):
+            piece = o_sb[t][:, half, :]
+            if engine is nc.scalar:
                 nc.scalar.activation(out=piece, in_=piece, func=RELU)
-                rows = out[128 * half:128 * half + 128, :]
-                if t < UNITS - 1:
-                    nc.sync.dma_start(out=rows[:, 512 * t + 128:512 * t + 640], in_=piece)
-                else:
-                    nc.sync.dma_start(out=rows[:, 3712:4096], in_=o_sb[t][:, half, 0:384])
-                    nc.sync.dma_start(out=rows[:, 0:128], in_=o_sb[t][:, half, 384:512])
+            else:
+                nc.vector.tensor_scalar_max(piece, piece, 0.0)
+            store(t, half)
 
         transpose_inputs(0)
         copy_inputs(0)
@@ -220,25 +230,44 @@ def tile_capsuleneuralnetwork_pa_kernel(tc, primary_input, prev, col, W0, b0, W1
         quantise_weights(2)
         transpose_inputs(1)
         copy_inputs(1)
-        quantise_inputs(1)
 
-        for s in range(UNITS + LAG_OUT):
-            if s + AHEAD_X < UNITS:
-                transpose_inputs(s + AHEAD_X)
-                copy_inputs(s + AHEAD_X)
-            if s < UNITS:
-                layer1(s)
-            if 0 <= s - LAG_G < UNITS:
-                regroup_h(s - LAG_G)
+        for s in range(UNITS):
+            if s + 2 < UNITS:
+                transpose_inputs(s + 2)
+                copy_inputs(s + 2)
+            layer1(s)
+            if s >= 1:
+                regroup_h(s - 1)
+            if s >= 3:
+                add_bias(s - 3, 0)
+            if s >= 1:
+                roll_h(s - 1)
+            if s >= 3:
+                add_bias(s - 3, 1)
+            if s >= 2:
+                quantise_h(s - 2)
+            if s >= 3:
+                finish(s - 3, 0, nc.vector)
+                finish(s - 3, 1, nc.scalar)
+            relu_h(s)
+            if s + 1 < UNITS:
+                quantise_inputs(s + 1)
             if s == 0:
                 regroup_weights(3)
-            if 0 <= s - LAG_H < UNITS:
-                quantise_h(s - LAG_H)
-            if s + AHEAD_X < UNITS:
-                quantise_inputs(s + AHEAD_X)
-            if s == 0:
+            if s == 1:
                 quantise_weights(3)
-            if 0 <= s - LAG_H < UNITS:
-                layer2(s - LAG_H)
-            if 0 <= s - LAG_OUT < UNITS:
-                finish(s - LAG_OUT)
+            if s >= 2:
+                layer2(s - 2)
+
+        add_bias(5, 0)
+        add_bias(5, 1)
+        finish(5, 0, nc.scalar)
+        finish(5, 1, nc.scalar)
+        regroup_and_roll_last_h()
+        quantise_h(6)
+        quantise_h(7)
+        for t in (6, 7):
+            layer2(t)
+            for half in range(2):
+                add_bias(t, half)
+                finish(t, half, nc.scalar)

@@ -106,8 +106,8 @@ def tile_capsuleneuralnetwork_pa_kernel(tc, primary_input, prev, col, W0, b0, W1
         accs = {}
         ys = {}
 
-        def transpose_inputs(t):
-            for g in range(PASSES):
+        def transpose_inputs(t, passes=range(PASSES)):
+            for g in passes:
                 words = (prim[t] if g < 2 else prv[t])[:].bitcast(F32)
                 base = 256 * g if g < 2 else 0
                 bank = ps_t.tile([128, 2, 2, 128], F32, name="bank", tag="tp")
@@ -232,32 +232,36 @@ def tile_capsuleneuralnetwork_pa_kernel(tc, primary_input, prev, col, W0, b0, W1
         copy_inputs(1)
 
         for s in range(UNITS):
-            if s + 2 < UNITS:
-                transpose_inputs(s + 2)
-                copy_inputs(s + 2)
             layer1(s)
-            if s >= 1:
-                regroup_h(s - 1)
+            relu_h(s)
+            if s + 2 < UNITS:
+                transpose_inputs(s + 2, (0, 1))
             if s >= 3:
                 add_bias(s - 3, 0)
             if s >= 1:
-                roll_h(s - 1)
+                regroup_h(s - 1)
             if s >= 3:
                 add_bias(s - 3, 1)
+            if s >= 1:
+                roll_h(s - 1)
+            if s + 1 < UNITS:
+                quantise_inputs(s + 1, (0,))
             if s >= 2:
                 quantise_h(s - 2)
             if s >= 3:
                 finish(s - 3, 0, nc.vector)
                 finish(s - 3, 1, nc.scalar)
-            relu_h(s)
             if s + 1 < UNITS:
-                quantise_inputs(s + 1)
+                quantise_inputs(s + 1, (1, 2))
             if s == 0:
                 regroup_weights(3)
             if s == 1:
                 quantise_weights(3)
             if s >= 2:
                 layer2(s - 2)
+            if s + 2 < UNITS:
+                transpose_inputs(s + 2, (2,))
+                copy_inputs(s + 2)
 
         add_bias(5, 0)
         add_bias(5, 1)

@@ -41,10 +41,8 @@ def tile_capsuleneuralnetwork_pa_kernel(tc, primary_input, prev, col, W0, b0, W1
         col_sb = keep.tile([1, 1], BF16, name="col_sb")
         nc.scalar.dma_start(out=col_sb[0:1, 0:1], in_=col.unsqueeze(0))
         nc.gpsimd.tensor_copy(out=col_ones[0:1, :], in_=col_sb[0:1, 0:1].to_broadcast([1, 128]))
-        nc.scalar.dma_start(out=bias_rows[0:1, 0:384], in_=W0[1536:1537, 128:512])
-        nc.scalar.dma_start(out=bias_rows[0:1, 384:512], in_=W0[1536:1537, 0:128])
-        nc.scalar.dma_start(out=bias_rows[32:33, 0:384], in_=b0[128:512].unsqueeze(0))
-        nc.scalar.dma_start(out=bias_rows[32:33, 384:512], in_=b0[0:128].unsqueeze(0))
+        nc.scalar.dma_start(out=bias_rows[0:1, 0:512], in_=W0[1536:1537, :])
+        nc.scalar.dma_start(out=bias_rows[32:33, 0:512], in_=b0.unsqueeze(0))
         nc.scalar.dma_start(out=bias_rows[0:1, 512:1024], in_=W1[512:513, :])
         nc.scalar.dma_start(out=bias_rows[32:33, 512:1024], in_=b1.unsqueeze(0))
 
@@ -64,7 +62,9 @@ def tile_capsuleneuralnetwork_pa_kernel(tc, primary_input, prev, col, W0, b0, W1
             nc.sync.dma_start(out=w_raw[g][:], in_=W0[512 * g:512 * g + 512, :].rearrange("(p j) c -> p j c", j=4))
 
         def load_w1():
-            nc.sync.dma_start(out=w_raw[3][:], in_=W1[0:512, :].rearrange("(p j) n -> p j n", j=4))
+            rows = W1[0:512, :].rearrange("(c j i) n -> j c i n", j=4, i=4)
+            for j in range(4):
+                nc.sync.dma_start(out=w_raw[3][:, j, :], in_=rows[j])
 
         load_primary(0)
         load_w0(0)
@@ -132,18 +132,28 @@ def tile_capsuleneuralnetwork_pa_kernel(tc, primary_input, prev, col, W0, b0, W1
             if g == 3:
                 regroup(w_g[g][:], w_raw[g][:])
                 return
-            dst = w_g[g][:].rearrange("p (t m j) -> p t m j", t=4, j=4)
-            src = w_raw[g][:].rearrange("p j (m t) -> p t m j", t=4)
-            nc.vector.tensor_copy(out=dst[:, :, 0:96, :], in_=src[:, :, 32:128, :])
-            nc.vector.tensor_copy(out=dst[:, :, 96:128, :], in_=src[:, :, 0:32, :])
+            dst = w_g[g][:].rearrange("p (t c i j) -> p t c j i", t=4, c=32, i=4, j=4)
+            src = w_raw[g][:].rearrange("p j (c t i) -> p t c j i", c=32, t=4, i=4)
+            for (c0, c1, r0) in ((0, 24, 8), (24, 32, 0)):
+                for t in range(4):
+                    copy = nc.scalar.copy if g == 2 and t >= 2 else nc.vector.tensor_copy
+                    copy(out=dst[:, t, c0:c1], in_=src[:, t, r0:r0 + c1 - c0])
 
         def quantise_weights(g):
             quantise(w_c[g][:], w_s[g][:], w_g[g][:])
 
+        rolled = keep.tile([128, 512], BF16, name="rolled")
+
+        def roll_bias_rows():
+            dst = rolled[:].rearrange("p (j c i) -> p j c i", j=4, i=4)
+            src = bias_rows[:, 0:512].rearrange("p (c j i) -> p j c i", j=4, i=4)
+            nc.scalar.copy(out=dst[:, :, 0:24, :], in_=src[:, :, 8:32, :])
+            nc.scalar.copy(out=dst[:, :, 24:32, :], in_=src[:, :, 0:8, :])
+
         def biases():
             pb0 = ps_y.tile([128, 4, 64], F32, name="pb0", tag="y")
             for j in range(4):
-                nc.tensor.matmul(out=pb0[:, j, :], lhsT=bias_rows[:, j:512:4], rhs=col_ones[:, 0:64],
+                nc.tensor.matmul(out=pb0[:, j, :], lhsT=rolled[:, 128 * j:128 * j + 128], rhs=col_ones[:, 0:64],
                                  start=True, stop=True)
             nc.scalar.copy(out=bias0[:], in_=pb0[:, :, 0])
             pb1 = ps_y.tile([128, 512], F32, name="pb1", tag="y")
@@ -178,12 +188,43 @@ def tile_capsuleneuralnetwork_pa_kernel(tc, primary_input, prev, col, W0, b0, W1
         def roll_h(t):
             nc.vector.tensor_copy(out=h_g[(t - 1) % UNITS][96:128, :], in_=h_g[t][96:128, :])
 
-        def regroup_and_roll_last_h():
-            regroup(h_g[UNITS - 2][96:128, :], h_t[UNITS - 1][96:128])
-            regroup(h_g[UNITS - 1][0:96, :], h_t[UNITS - 1][0:96])
+        def layer1_half(t, half):
+            acc = ps_a.tile([128, 4, 128], F32, name="acc_half", tag="acc")
+            accs[(t, half)] = acc
+            cols = slice(128 * half, 128 * half + 128)
+            for j in range(4):
+                for g in range(PASSES):
+                    nc.tensor.matmul_mx(
+                        out=acc[:, j, :],
+                        lhsT=w_c[g][:, 128 * j:128 * j + 128].bitcast(FP8X4),
+                        lhsT_scale=w_s[g][:, 128 * j:128 * j + 128],
+                        rhs=x_c[t][:, g, cols].bitcast(FP8X4),
+                        rhs_scale=x_s[t][:, g, cols],
+                        start=(g == 0),
+                        stop=(g == PASSES - 1),
+                    )
+
+        def relu_h_half(t, half):
+            cols = slice(128 * half, 128 * half + 128)
+            for j in range(2):
+                nc.scalar.activation(out=h_t[t][:, j, cols], in_=accs[(t, half)][:, j, :], func=RELU,
+                                     bias=bias0[:, j:j + 1], scale=1.0)
+            for j in range(2, 4):
+                nc.vector.tensor_scalar(out=h_t[t][:, j, cols], in0=accs[(t, half)][:, j, :],
+                                        scalar1=bias0[:, j:j + 1], scalar2=0.0, op0=ADD,
+                                        op1=mybir.AluOpType.max)
+
+        def regroup_and_roll_last_h(half):
+            cols, words = slice(128 * half, 128 * half + 128), slice(512 * half, 512 * half + 512)
+            regroup(h_g[UNITS - 2][96:128, words], h_t[UNITS - 1][96:128, :, cols])
+            regroup(h_g[UNITS - 1][0:96, words], h_t[UNITS - 1][0:96, :, cols])
 
         def quantise_h(t):
             quantise(h_c[t][:], h_s[t][:], h_g[t][:])
+
+        def quantise_h_half(t, half):
+            cols = slice(128 * half, 128 * half + 128)
+            quantise(h_c[t][:, cols], h_s[t][:, cols], h_g[t][:, 512 * half:512 * half + 512])
 
         def store(t, half):
             rows = out[128 * half:128 * half + 128, :]
@@ -193,8 +234,8 @@ def tile_capsuleneuralnetwork_pa_kernel(tc, primary_input, prev, col, W0, b0, W1
                 nc.sync.dma_start(out=rows[:, 3712:4096], in_=o_sb[t][:, half, 0:384])
                 nc.sync.dma_start(out=rows[:, 0:128], in_=o_sb[t][:, half, 384:512])
 
-        def layer2(t):
-            for half in range(2):
+        def layer2(t, halves=(0, 1)):
+            for half in halves:
                 y = ps_y.tile([128, 512], F32, name="y", tag="y")
                 ys[(t, half)] = y
                 nc.tensor.matmul_mx(
@@ -220,58 +261,71 @@ def tile_capsuleneuralnetwork_pa_kernel(tc, primary_input, prev, col, W0, b0, W1
 
         transpose_inputs(0)
         copy_inputs(0)
-        biases()
         regroup_weights(0)
-        regroup_weights(1)
+        quantise_inputs(0, (0,))
         quantise_weights(0)
-        quantise_inputs(0)
+        regroup_weights(1)
+        quantise_inputs(0, (1, 2))
         regroup_weights(2)
         quantise_weights(1)
         quantise_weights(2)
+        roll_bias_rows()
         transpose_inputs(1)
         copy_inputs(1)
+        biases()
 
-        for s in range(UNITS):
+        for s in range(UNITS - 1):
             layer1(s)
             relu_h(s)
             if s + 2 < UNITS:
-                transpose_inputs(s + 2, (0, 1))
-            if s >= 3:
-                add_bias(s - 3, 0)
+                transpose_inputs(s + 2)
+                copy_inputs(s + 2)
             if s >= 1:
                 regroup_h(s - 1)
             if s >= 3:
-                add_bias(s - 3, 1)
+                add_bias(s - 3, 0)
             if s >= 1:
                 roll_h(s - 1)
-            if s + 1 < UNITS:
-                quantise_inputs(s + 1, (0,))
+            if s >= 3:
+                add_bias(s - 3, 1)
+            quantise_inputs(s + 1, (0,))
             if s >= 2:
                 quantise_h(s - 2)
             if s >= 3:
                 finish(s - 3, 0, nc.vector)
                 finish(s - 3, 1, nc.scalar)
-            if s + 1 < UNITS:
-                quantise_inputs(s + 1, (1, 2))
+            quantise_inputs(s + 1, (1, 2))
             if s == 0:
                 regroup_weights(3)
             if s == 1:
                 quantise_weights(3)
             if s >= 2:
                 layer2(s - 2)
-            if s + 2 < UNITS:
-                transpose_inputs(s + 2, (2,))
-                copy_inputs(s + 2)
 
+        layer1_half(7, 0)
+        layer1_half(7, 1)
+        regroup_h(6)
+        add_bias(4, 0)
+        roll_h(6)
+        add_bias(4, 1)
+        quantise_h(5)
+        layer2(5)
+        relu_h_half(7, 0)
+        regroup_and_roll_last_h(0)
+        relu_h_half(7, 1)
+        quantise_h_half(6, 0)
+        quantise_h_half(7, 0)
+        regroup_and_roll_last_h(1)
+        finish(4, 0, nc.scalar)
+        finish(4, 1, nc.scalar)
         add_bias(5, 0)
+        quantise_h_half(6, 1)
         add_bias(5, 1)
+        quantise_h_half(7, 1)
         finish(5, 0, nc.scalar)
         finish(5, 1, nc.scalar)
-        regroup_and_roll_last_h()
-        quantise_h(6)
-        quantise_h(7)
-        for t in (6, 7):
-            layer2(t)
-            for half in range(2):
+        for half in range(2):
+            for t in (6, 7):
+                layer2(t, (half,))
                 add_bias(t, half)
                 finish(t, half, nc.scalar)

@@ -135,9 +135,11 @@ def tile_capsuleneuralnetwork_pa_kernel(tc, primary_input, prev, col, W0, b0, W1
             dst = w_g[g][:].rearrange("p (t c i j) -> p t c j i", t=4, c=32, i=4, j=4)
             src = w_raw[g][:].rearrange("p j (c t i) -> p t c j i", c=32, t=4, i=4)
             for (c0, c1, r0) in ((0, 24, 8), (24, 32, 0)):
-                for t in range(4):
-                    copy = nc.scalar.copy if g == 2 and t >= 2 else nc.vector.tensor_copy
-                    copy(out=dst[:, t, c0:c1], in_=src[:, t, r0:r0 + c1 - c0])
+                if g < 2:
+                    nc.vector.tensor_copy(out=dst[:, :, c0:c1], in_=src[:, :, r0:r0 + c1 - c0])
+                else:
+                    nc.vector.tensor_copy(out=dst[:, 0:2, c0:c1], in_=src[:, 0:2, r0:r0 + c1 - c0])
+                    nc.scalar.copy(out=dst[:, 2:4, c0:c1], in_=src[:, 2:4, r0:r0 + c1 - c0])
 
         def quantise_weights(g):
             quantise(w_c[g][:], w_s[g][:], w_g[g][:])
@@ -151,12 +153,12 @@ def tile_capsuleneuralnetwork_pa_kernel(tc, primary_input, prev, col, W0, b0, W1
             nc.scalar.copy(out=dst[:, :, 24:32, :], in_=src[:, :, 0:8, :])
 
         def biases():
-            pb0 = ps_y.tile([128, 4, 64], F32, name="pb0", tag="y")
+            pb0 = ps_t.tile([128, 4, 64], F32, name="pb0", tag="tp")
             for j in range(4):
                 nc.tensor.matmul(out=pb0[:, j, :], lhsT=rolled[:, 128 * j:128 * j + 128], rhs=col_ones[:, 0:64],
                                  start=True, stop=True)
             nc.scalar.copy(out=bias0[:], in_=pb0[:, :, 0])
-            pb1 = ps_y.tile([128, 512], F32, name="pb1", tag="y")
+            pb1 = ps_t.tile([128, 512], F32, name="pb1", tag="tp")
             nc.tensor.matmul(out=pb1[:], lhsT=col_ones[:], rhs=bias_rows[:, 512:1024], start=True, stop=True)
             nc.scalar.copy(out=bias1[:], in_=pb1[:])
 
@@ -177,9 +179,53 @@ def tile_capsuleneuralnetwork_pa_kernel(tc, primary_input, prev, col, W0, b0, W1
                             stop=(g == PASSES - 1),
                         )
 
+        def layer1_first(g):
+            for j in range(4):
+                if g == 0:
+                    pool, tag = (ps_a, "acc") if j < 3 else (ps_y, "y")
+                    first = pool.tile([128, 512], F32, name="first", tag=tag)
+                    accs[(0, j)] = first
+                nc.tensor.matmul_mx(
+                    out=accs[(0, j)][:, 0:256],
+                    lhsT=w_c[g][:, 128 * j:128 * j + 128].bitcast(FP8X4),
+                    lhsT_scale=w_s[g][:, 128 * j:128 * j + 128],
+                    rhs=x_c[0][:, g, :].bitcast(FP8X4),
+                    rhs_scale=x_s[0][:, g, :],
+                    start=(g == 0),
+                    stop=(g == PASSES - 1),
+                )
+
         def relu_h(t):
             for j in range(4):
-                nc.scalar.activation(out=h_t[t][:, j, :], in_=accs[(t, j // 2)][:, j % 2, :], func=RELU,
+                src = accs[(t, j)][:, 0:256] if t == 0 else accs[(t, j // 2)][:, j % 2, :]
+                nc.scalar.activation(out=h_t[t][:, j, :], in_=src, func=RELU, bias=bias0[:, j:j + 1], scale=1.0)
+
+        def regroup_h(t):
+            regroup(h_g[t][:], h_t[t][:])
+
+        def roll_h(t):
+            nc.vector.tensor_copy(out=h_g[(t - 1) % UNITS][96:128, :], in_=h_g[t][96:128, :])
+
+        def layer1_half(t, half):
+            acc = ps_a.tile([128, 4, 128], F32, name="acc_half", tag="acc")
+            accs[(t, half)] = acc
+            cols = slice(128 * half, 128 * half + 128)
+            for j in range(4):
+                for g in range(PASSES):
+                    nc.tensor.matmul_mx(
+                        out=acc[:, j, :],
+                        lhsT=w_c[g][:, 128 * j:128 * j + 128].bitcast(FP8X4),
+                        lhsT_scale=w_s[g][:, 128 * j:128 * j + 128],
+                        rhs=x_c[t][:, g, cols].bitcast(FP8X4),
+                        rhs_scale=x_s[t][:, g, cols],
+                        start=(g == 0),
+                        stop=(g == PASSES - 1),
+                    )
+
+        def relu_h_half(t, half):
+            cols = slice(128 * half, 128 * half + 128)
+            for j in range(4):
+                nc.scalar.activation(out=h_t[t][:, j, cols], in_=accs[(t, half)][:, j, :], func=RELU,
                                      bias=bias0[:, j:j + 1], scale=1.0)
 
         def regroup_h(t):
@@ -234,9 +280,9 @@ def tile_capsuleneuralnetwork_pa_kernel(tc, primary_input, prev, col, W0, b0, W1
                 nc.sync.dma_start(out=rows[:, 3712:4096], in_=o_sb[t][:, half, 0:384])
                 nc.sync.dma_start(out=rows[:, 0:128], in_=o_sb[t][:, half, 384:512])
 
-        def layer2(t, halves=(0, 1)):
+        def layer2(t, halves=(0, 1), pool=ps_y, tag="y"):
             for half in halves:
-                y = ps_y.tile([128, 512], F32, name="y", tag="y")
+                y = pool.tile([128, 512], F32, name="y", tag=tag)
                 ys[(t, half)] = y
                 nc.tensor.matmul_mx(
                     out=y[:],
@@ -264,68 +310,82 @@ def tile_capsuleneuralnetwork_pa_kernel(tc, primary_input, prev, col, W0, b0, W1
         regroup_weights(0)
         quantise_inputs(0, (0,))
         quantise_weights(0)
+        layer1_first(0)
         regroup_weights(1)
-        quantise_inputs(0, (1, 2))
-        regroup_weights(2)
+        quantise_inputs(0, (1,))
         quantise_weights(1)
-        quantise_weights(2)
+        layer1_first(1)
+        regroup_weights(2)
         roll_bias_rows()
+        biases()
+        quantise_inputs(0, (2,))
+        quantise_weights(2)
         transpose_inputs(1)
         copy_inputs(1)
-        biases()
+        layer1_first(2)
 
         for s in range(UNITS - 1):
-            layer1(s)
+            if s > 0:
+                layer1(s)
             relu_h(s)
             if s + 2 < UNITS:
-                transpose_inputs(s + 2)
-                copy_inputs(s + 2)
-            if s >= 1:
-                regroup_h(s - 1)
-            if s >= 3:
-                add_bias(s - 3, 0)
+                transpose_inputs(s + 2, (0,))
             if s >= 1:
                 roll_h(s - 1)
-            if s >= 3:
-                add_bias(s - 3, 1)
             quantise_inputs(s + 1, (0,))
             if s >= 2:
                 quantise_h(s - 2)
-            if s >= 3:
-                finish(s - 3, 0, nc.vector)
-                finish(s - 3, 1, nc.scalar)
             quantise_inputs(s + 1, (1, 2))
             if s == 0:
                 regroup_weights(3)
             if s == 1:
                 quantise_weights(3)
+            if s >= 3:
+                finish(s - 3, 0, nc.vector if s < 6 else nc.scalar)
+                finish(s - 3, 1, nc.scalar)
             if s >= 2:
                 layer2(s - 2)
+            if s + 2 < UNITS:
+                transpose_inputs(s + 2, (1, 2))
+                copy_inputs(s + 2)
+            regroup_h(s)
+            if s >= 2:
+                add_bias(s - 2, 0)
+            if s == 6:
+                roll_h(6)
+            if s >= 2:
+                add_bias(s - 2, 1)
 
         layer1_half(7, 0)
         layer1_half(7, 1)
-        regroup_h(6)
-        add_bias(4, 0)
-        roll_h(6)
-        add_bias(4, 1)
+        relu_h_half(7, 0)
+        relu_h_half(7, 1)
         quantise_h(5)
         layer2(5)
-        relu_h_half(7, 0)
-        regroup_and_roll_last_h(0)
-        relu_h_half(7, 1)
-        quantise_h_half(6, 0)
-        quantise_h_half(7, 0)
-        regroup_and_roll_last_h(1)
         finish(4, 0, nc.scalar)
         finish(4, 1, nc.scalar)
+        regroup_and_roll_last_h(0)
         add_bias(5, 0)
-        quantise_h_half(6, 1)
+        quantise_h_half(6, 0)
+        quantise_h_half(7, 0)
+        layer2(6, (0,), ps_t, "tp")
+        layer2(7, (0,), ps_t, "tp")
+        regroup_and_roll_last_h(1)
         add_bias(5, 1)
+        quantise_h_half(6, 1)
         quantise_h_half(7, 1)
+        layer2(6, (1,), ps_t, "tp")
+        layer2(7, (1,))
         finish(5, 0, nc.scalar)
         finish(5, 1, nc.scalar)
-        for half in range(2):
-            for t in (6, 7):
-                layer2(t, (half,))
-                add_bias(t, half)
-                finish(t, half, nc.scalar)
+        for (t, half) in ((6, 0), (7, 0), (6, 1)):
+            add_bias(t, half)
+            finish(t, half, nc.scalar)
+        for (a, b, engine) in ((0, 256, nc.scalar), (256, 512, nc.vector)):
+            piece = o_sb[7][:, 1, a:b]
+            nc.vector.tensor_tensor(out=piece, in0=ys[(7, 1)][:, a:b], in1=bias1[:, a:b], op=ADD)
+            if engine is nc.scalar:
+                nc.scalar.activation(out=piece, in_=piece, func=RELU)
+            else:
+                nc.vector.tensor_scalar_max(piece, piece, 0.0)
+        store(7, 1)

@@ -21,7 +21,7 @@ def tile_capsuleneuralnetwork_pa_kernel(tc, primary_input, prev, col, W0, b0, W1
     nc = tc.nc
     with ExitStack() as ctx:
         keep = ctx.enter_context(tc.tile_pool(name="keep", bufs=1))
-        stage = ctx.enter_context(tc.tile_pool(name="stage", bufs=6))
+        stage = ctx.enter_context(tc.tile_pool(name="stage", bufs=2))
         ps_t = ctx.enter_context(tc.psum_pool(name="ps_t", bufs=3))
         ps_a = ctx.enter_context(tc.psum_pool(name="ps_a", bufs=3))
         ps_y = ctx.enter_context(tc.psum_pool(name="ps_y", bufs=2))
@@ -117,16 +117,24 @@ def tile_capsuleneuralnetwork_pa_kernel(tc, primary_input, prev, col, W0, b0, W1
                         nc.tensor.transpose(bank[:, half, e, :], words[:, half, base + e:base + 256:2], ident[:])
 
         def copy_inputs(t):
-            for g in range(PASSES):
-                grp = stage.tile([128, 1024], BF16, name="x_g", tag="x_g", align_bytes=64)
-                x_g[(t, g)] = grp
-                dst = grp[:].bitcast(F32).rearrange("p (t b h) -> p t b h", t=2, b=128, h=2)
+            both = stage.tile([128, 2048], BF16, name="x_g01", tag="x_g01", align_bytes=64)
+            last = stage.tile([128, 1024], BF16, name="x_g2", tag="x_g2", align_bytes=64)
+            x_g[t] = (both, last)
+            for g, grp in ((0, both[:, 0:1024]), (1, both[:, 1024:2048]), (2, last[:])):
+                dst = grp.bitcast(F32).rearrange("p (t b h) -> p t b h", t=2, b=128, h=2)
                 src = banks[(t, g)][:].rearrange("p t h b -> p t b h")
                 nc.scalar.copy(out=dst, in_=src)
 
-        def quantise_inputs(t, passes=range(PASSES)):
-            for g in passes:
-                quantise(x_c[t][:, g, :], x_s[t][:, g, :], x_g[(t, g)][:])
+        def quantise_inputs(t, passes):
+            both, last = x_g[t]
+            if passes == (0, 1):
+                quantise(x_c[t][:, 0:2, :].rearrange("p g n -> p (g n)"),
+                         x_s[t][:, 0:2, :].rearrange("p g n -> p (g n)"), both[:])
+            elif passes == (2,):
+                quantise(x_c[t][:, 2, :], x_s[t][:, 2, :], last[:])
+            else:
+                (g,) = passes
+                quantise(x_c[t][:, g, :], x_s[t][:, g, :], both[:, 1024 * g:1024 * g + 1024])
 
         def regroup_weights(g):
             if g == 3:
@@ -332,17 +340,17 @@ def tile_capsuleneuralnetwork_pa_kernel(tc, primary_input, prev, col, W0, b0, W1
                 transpose_inputs(s + 2, (0,))
             if s >= 1:
                 roll_h(s - 1)
-            quantise_inputs(s + 1, (0,))
+            quantise_inputs(s + 1, (0, 1))
             if s >= 2:
                 quantise_h(s - 2)
-            quantise_inputs(s + 1, (1, 2))
+            quantise_inputs(s + 1, (2,))
             if s == 0:
                 regroup_weights(3)
             if s == 1:
                 quantise_weights(3)
             if s >= 3:
                 finish(s - 3, 0, nc.vector if s < 6 else nc.scalar)
-                finish(s - 3, 1, nc.scalar)
+                finish(s - 3, 1, nc.vector if s < 6 else nc.scalar)
             if s >= 2:
                 layer2(s - 2)
             if s + 2 < UNITS:

@@ -27,10 +27,6 @@ def tile_capsuleneuralnetwork_pa_kernel(tc, primary_input, prev, col, W0, b0, W1
         ps_y = ctx.enter_context(tc.psum_pool(name="ps_y", bufs=2))
         ctx.enter_context(tc.manual_schedule())
 
-        warm = keep.tile([128, 1], F32, name="warm")
-        nc.gpsimd.memset(warm[:], 0.0)
-        nc.scalar.activation(out=warm[:], in_=warm[:], func=RELU)
-
         ident = keep.tile([128, 128], F32, name="ident")
         make_identity(nc, ident[:])
         bias_rows = keep.tile([128, 1024], BF16, name="bias_rows")
@@ -45,6 +41,10 @@ def tile_capsuleneuralnetwork_pa_kernel(tc, primary_input, prev, col, W0, b0, W1
         nc.scalar.dma_start(out=bias_rows[32:33, 0:512], in_=b0.unsqueeze(0))
         nc.scalar.dma_start(out=bias_rows[0:1, 512:1024], in_=W1[512:513, :])
         nc.scalar.dma_start(out=bias_rows[32:33, 512:1024], in_=b1.unsqueeze(0))
+
+        warm = keep.tile([128, 1], F32, name="warm")
+        nc.gpsimd.memset(warm[:], 0.0)
+        nc.scalar.activation(out=warm[:], in_=warm[:], func=RELU)
 
         prim = [keep.tile([128, 2, 1024], BF16, name="prim%d" % u) for u in range(UNITS)]
         prv = [keep.tile([128, 2, 512], BF16, name="prv%d" % u) for u in range(UNITS)]
@@ -71,11 +71,10 @@ def tile_capsuleneuralnetwork_pa_kernel(tc, primary_input, prev, col, W0, b0, W1
         load_prev(0)
         load_w0(1)
         load_w0(2)
-        for t in (1, 2):
-            load_primary(t)
-            load_prev(t)
+        load_primary(1)
+        load_prev(1)
         load_w1()
-        for t in range(3, UNITS):
+        for t in range(2, UNITS):
             load_primary(t)
             load_prev(t)
 
@@ -92,8 +91,8 @@ def tile_capsuleneuralnetwork_pa_kernel(tc, primary_input, prev, col, W0, b0, W1
         bias0 = keep.tile([128, 4], F32, name="bias0")
         bias1 = keep.tile([128, 512], F32, name="bias1")
 
-        def regroup(dst, src):
-            nc.vector.tensor_copy(
+        def regroup(dst, src, copy=nc.vector.tensor_copy):
+            copy(
                 out=dst.rearrange("p (c i t) -> p c t i", i=4, t=4),
                 in_=src.rearrange("p t (c i) -> p c t i", i=4),
             )
@@ -116,11 +115,14 @@ def tile_capsuleneuralnetwork_pa_kernel(tc, primary_input, prev, col, W0, b0, W1
                     for e in range(2):
                         nc.tensor.transpose(bank[:, half, e, :], words[:, half, base + e:base + 256:2], ident[:])
 
-        def copy_inputs(t):
-            both = stage.tile([128, 2048], BF16, name="x_g01", tag="x_g01", align_bytes=64)
-            last = stage.tile([128, 1024], BF16, name="x_g2", tag="x_g2", align_bytes=64)
-            x_g[t] = (both, last)
-            for g, grp in ((0, both[:, 0:1024]), (1, both[:, 1024:2048]), (2, last[:])):
+        def copy_inputs(t, passes=range(PASSES)):
+            if 0 in passes:
+                both = stage.tile([128, 2048], BF16, name="x_g01", tag="x_g01", align_bytes=64)
+                last = stage.tile([128, 1024], BF16, name="x_g2", tag="x_g2", align_bytes=64)
+                x_g[t] = (both, last)
+            both, last = x_g[t]
+            for g in passes:
+                grp = both[:, 1024 * g:1024 * g + 1024] if g < 2 else last[:]
                 dst = grp.bitcast(F32).rearrange("p (t b h) -> p t b h", t=2, b=128, h=2)
                 src = banks[(t, g)][:].rearrange("p t h b -> p t b h")
                 nc.scalar.copy(out=dst, in_=src)
@@ -208,11 +210,11 @@ def tile_capsuleneuralnetwork_pa_kernel(tc, primary_input, prev, col, W0, b0, W1
                 src = accs[(t, j)][:, 0:256] if t == 0 else accs[(t, j // 2)][:, j % 2, :]
                 nc.scalar.activation(out=h_t[t][:, j, :], in_=src, func=RELU, bias=bias0[:, j:j + 1], scale=1.0)
 
-        def regroup_h(t):
-            regroup(h_g[t][:], h_t[t][:])
+        def regroup_h(t, copy=nc.vector.tensor_copy):
+            regroup(h_g[t][:], h_t[t][:], copy)
 
-        def roll_h(t):
-            nc.vector.tensor_copy(out=h_g[(t - 1) % UNITS][96:128, :], in_=h_g[t][96:128, :])
+        def roll_h(t, copy=nc.vector.tensor_copy):
+            copy(out=h_g[(t - 1) % UNITS][96:128, :], in_=h_g[t][96:128, :])
 
         def layer1_half(t, half):
             acc = ps_a.tile([128, 4, 128], F32, name="acc_half", tag="acc")
@@ -236,42 +238,10 @@ def tile_capsuleneuralnetwork_pa_kernel(tc, primary_input, prev, col, W0, b0, W1
                 nc.scalar.activation(out=h_t[t][:, j, cols], in_=accs[(t, half)][:, j, :], func=RELU,
                                      bias=bias0[:, j:j + 1], scale=1.0)
 
-        def regroup_h(t):
-            regroup(h_g[t][:], h_t[t][:])
-
-        def roll_h(t):
-            nc.vector.tensor_copy(out=h_g[(t - 1) % UNITS][96:128, :], in_=h_g[t][96:128, :])
-
-        def layer1_half(t, half):
-            acc = ps_a.tile([128, 4, 128], F32, name="acc_half", tag="acc")
-            accs[(t, half)] = acc
-            cols = slice(128 * half, 128 * half + 128)
-            for j in range(4):
-                for g in range(PASSES):
-                    nc.tensor.matmul_mx(
-                        out=acc[:, j, :],
-                        lhsT=w_c[g][:, 128 * j:128 * j + 128].bitcast(FP8X4),
-                        lhsT_scale=w_s[g][:, 128 * j:128 * j + 128],
-                        rhs=x_c[t][:, g, cols].bitcast(FP8X4),
-                        rhs_scale=x_s[t][:, g, cols],
-                        start=(g == 0),
-                        stop=(g == PASSES - 1),
-                    )
-
-        def relu_h_half(t, half):
-            cols = slice(128 * half, 128 * half + 128)
-            for j in range(2):
-                nc.scalar.activation(out=h_t[t][:, j, cols], in_=accs[(t, half)][:, j, :], func=RELU,
-                                     bias=bias0[:, j:j + 1], scale=1.0)
-            for j in range(2, 4):
-                nc.vector.tensor_scalar(out=h_t[t][:, j, cols], in0=accs[(t, half)][:, j, :],
-                                        scalar1=bias0[:, j:j + 1], scalar2=0.0, op0=ADD,
-                                        op1=mybir.AluOpType.max)
-
-        def regroup_and_roll_last_h(half):
+        def regroup_and_roll_last_h(half, copy=nc.vector.tensor_copy):
             cols, words = slice(128 * half, 128 * half + 128), slice(512 * half, 512 * half + 512)
             regroup(h_g[UNITS - 2][96:128, words], h_t[UNITS - 1][96:128, :, cols])
-            regroup(h_g[UNITS - 1][0:96, words], h_t[UNITS - 1][0:96, :, cols])
+            regroup(h_g[UNITS - 1][0:96, words], h_t[UNITS - 1][0:96, :, cols], copy)
 
         def quantise_h(t):
             quantise(h_c[t][:], h_s[t][:], h_g[t][:])
@@ -314,7 +284,10 @@ def tile_capsuleneuralnetwork_pa_kernel(tc, primary_input, prev, col, W0, b0, W1
             store(t, half)
 
         transpose_inputs(0)
-        copy_inputs(0)
+        copy_inputs(0, (0, 1))
+        roll_bias_rows()
+        copy_inputs(0, (2,))
+        biases()
         regroup_weights(0)
         quantise_inputs(0, (0,))
         quantise_weights(0)
@@ -324,15 +297,19 @@ def tile_capsuleneuralnetwork_pa_kernel(tc, primary_input, prev, col, W0, b0, W1
         quantise_weights(1)
         layer1_first(1)
         regroup_weights(2)
-        roll_bias_rows()
-        biases()
         quantise_inputs(0, (2,))
         quantise_weights(2)
-        transpose_inputs(1)
-        copy_inputs(1)
+        regroup_weights(3)
+        transpose_inputs(1, (0, 1))
+        copy_inputs(1, (0, 1))
         layer1_first(2)
+        transpose_inputs(1, (2,))
+        copy_inputs(1, (2,))
+        quantise_inputs(1, (0, 1))
+        quantise_weights(3)
+        quantise_inputs(1, (2,))
 
-        for s in range(UNITS - 1):
+        for s in range(UNITS - 2):
             if s > 0:
                 layer1(s)
             relu_h(s)
@@ -340,17 +317,15 @@ def tile_capsuleneuralnetwork_pa_kernel(tc, primary_input, prev, col, W0, b0, W1
                 transpose_inputs(s + 2, (0,))
             if s >= 1:
                 roll_h(s - 1)
-            quantise_inputs(s + 1, (0, 1))
+            if s >= 3:
+                finish(s - 3, 0, nc.vector)
+                finish(s - 3, 1, nc.scalar)
             if s >= 2:
                 quantise_h(s - 2)
-            quantise_inputs(s + 1, (2,))
-            if s == 0:
-                regroup_weights(3)
-            if s == 1:
-                quantise_weights(3)
-            if s >= 3:
-                finish(s - 3, 0, nc.vector if s < 6 else nc.scalar)
-                finish(s - 3, 1, nc.vector if s < 6 else nc.scalar)
+            if s > 0:
+                quantise_inputs(s + 1, (0, 1))
+            if s > 0:
+                quantise_inputs(s + 1, (2,))
             if s >= 2:
                 layer2(s - 2)
             if s + 2 < UNITS:
@@ -359,26 +334,37 @@ def tile_capsuleneuralnetwork_pa_kernel(tc, primary_input, prev, col, W0, b0, W1
             regroup_h(s)
             if s >= 2:
                 add_bias(s - 2, 0)
-            if s == 6:
-                roll_h(6)
             if s >= 2:
                 add_bias(s - 2, 1)
 
+        layer1(6)
+        relu_h(6)
+        roll_h(5)
+        finish(3, 0, nc.vector)
+        quantise_h(4)
+        quantise_inputs(7, (0, 1))
+        quantise_inputs(7, (2,))
+        layer2(4)
         layer1_half(7, 0)
         layer1_half(7, 1)
+        regroup_h(6)
+        add_bias(4, 0)
+        roll_h(6)
         relu_h_half(7, 0)
         relu_h_half(7, 1)
+        add_bias(4, 1)
         quantise_h(5)
         layer2(5)
-        finish(4, 0, nc.scalar)
-        finish(4, 1, nc.scalar)
         regroup_and_roll_last_h(0)
+        finish(3, 1, nc.scalar)
         add_bias(5, 0)
         quantise_h_half(6, 0)
         quantise_h_half(7, 0)
         layer2(6, (0,), ps_t, "tp")
         layer2(7, (0,), ps_t, "tp")
         regroup_and_roll_last_h(1)
+        finish(4, 0, nc.scalar)
+        finish(4, 1, nc.scalar)
         add_bias(5, 1)
         quantise_h_half(6, 1)
         quantise_h_half(7, 1)

@@ -7,6 +7,7 @@ F32 = mybir.dt.float32
 BF16 = mybir.dt.bfloat16
 U32 = mybir.dt.uint32
 U8 = mybir.dt.uint8
+I32 = mybir.dt.int32
 FP8X4 = mybir.dt.float8_e4m3fn_x4
 RELU = mybir.ActivationFunctionType.Relu
 ADD = mybir.AluOpType.add
@@ -41,22 +42,31 @@ def tile_capsuleneuralnetwork_pa_kernel(tc, primary_input, prev, col, W0, b0, W1
         nc.scalar.dma_start(out=bias_rows[32:33, 0:512], in_=b0.unsqueeze(0))
         nc.scalar.dma_start(out=bias_rows[0:1, 512:1024], in_=W1[512:513, :])
         nc.scalar.dma_start(out=bias_rows[32:33, 512:1024], in_=b1.unsqueeze(0))
-
         warm = keep.tile([128, 1], F32, name="warm")
         nc.gpsimd.memset(warm[:], 0.0)
         nc.scalar.activation(out=warm[:], in_=warm[:], func=RELU)
 
-        prim = [keep.tile([128, 2, 1024], BF16, name="prim%d" % u) for u in range(UNITS)]
-        prv = [keep.tile([128, 2, 512], BF16, name="prv%d" % u) for u in range(UNITS)]
+        own_c = keep.tile([128, 512], U32, name="own_c", align_bytes=64)
+        own_s = keep.tile([128, 512], U8, name="own_s", align_bytes=64)
+        next_c = keep.tile([128, 512], U32, name="next_c", align_bytes=64)
+        next_s = keep.tile([128, 512], U8, name="next_s", align_bytes=64)
+        nc.gpsimd.memset(own_c[96:128, :], 0)
+        nc.gpsimd.memset(next_c[0:96, :], 0)
+        nc.gpsimd.memset(own_s[:].bitcast(U32), 0)
+        nc.gpsimd.memset(next_s[:].bitcast(U32), 0)
+
+        prim = [keep.tile([128, 2048], BF16, name="prim%d" % u) for u in range(UNITS)]
+        prv = [keep.tile([128, 1024], BF16, name="prv%d" % u) for u in range(UNITS)]
         w_raw = [keep.tile([128, 4, 512], BF16, name="w_raw%d" % g) for g in range(4)]
 
-        def load_primary(t):
-            nc.sync.dma_start(out=prim[t][:],
-                              in_=primary_input[:, 1024 * t:1024 * t + 1024].rearrange("(h p) k -> p h k", h=2))
+        def load_primary(u):
+            half, v = divmod(u, 4)
+            nc.sync.dma_start(out=prim[u][:],
+                              in_=primary_input[128 * half:128 * half + 128, 2048 * v:2048 * v + 2048])
 
-        def load_prev(t):
-            nc.sync.dma_start(out=prv[t][:],
-                              in_=prev[:, 512 * t:512 * t + 512].rearrange("(h p) k -> p h k", h=2))
+        def load_prev(u):
+            half, v = divmod(u, 4)
+            nc.sync.dma_start(out=prv[u][:], in_=prev[128 * half:128 * half + 128, 1024 * v:1024 * v + 1024])
 
         def load_w0(g):
             nc.sync.dma_start(out=w_raw[g][:], in_=W0[512 * g:512 * g + 512, :].rearrange("(p j) c -> p j c", j=4))
@@ -73,26 +83,31 @@ def tile_capsuleneuralnetwork_pa_kernel(tc, primary_input, prev, col, W0, b0, W1
         load_w0(2)
         load_primary(1)
         load_prev(1)
+        load_primary(2)
+        load_prev(2)
         load_w1()
-        for t in range(2, UNITS):
-            load_primary(t)
-            load_prev(t)
+        for u in range(3, UNITS):
+            load_primary(u)
+            load_prev(u)
 
         w_g = [keep.tile([128, 2048], BF16, name="w_g%d" % g, align_bytes=64) for g in range(4)]
         w_c = [keep.tile([128, 512], U32, name="w_c%d" % g, align_bytes=64) for g in range(4)]
         w_s = [keep.tile([128, 512], U8, name="w_s%d" % g, align_bytes=64) for g in range(4)]
-        x_c = [keep.tile([128, PASSES, 256], U32, name="x_c%d" % t, align_bytes=64) for t in range(UNITS)]
-        x_s = [keep.tile([128, PASSES, 256], U8, name="x_s%d" % t, align_bytes=64) for t in range(UNITS)]
-        h_t = [keep.tile([128, 4, 256], BF16, name="h_t%d" % t) for t in range(UNITS)]
-        h_g = [keep.tile([128, 1024], BF16, name="h_g%d" % t, align_bytes=64) for t in range(UNITS)]
-        h_c = [keep.tile([128, 256], U32, name="h_c%d" % t, align_bytes=64) for t in range(UNITS)]
-        h_s = [keep.tile([128, 256], U8, name="h_s%d" % t, align_bytes=64) for t in range(UNITS)]
-        o_sb = [keep.tile([128, 2, 512], F32, name="o_sb%d" % t) for t in range(UNITS)]
+        x_c = [keep.tile([128, PASSES, 256], U32, name="x_c%d" % u, align_bytes=64) for u in range(UNITS)]
+        x_s = [keep.tile([128, PASSES, 256], U8, name="x_s%d" % u, align_bytes=64) for u in range(UNITS)]
+        h_t = [keep.tile([128, 4, 256], BF16, name="h_t%d" % u) for u in range(UNITS)]
+        h_g = [keep.tile([128, 4096], BF16, name="h_g%d" % h, align_bytes=64) for h in range(2)]
+        h_c = [keep.tile([128, 1024], U32, name="h_c%d" % h, align_bytes=64) for h in range(2)]
+        h_s = [keep.tile([128, 1024], U8, name="h_s%d" % h, align_bytes=64) for h in range(2)]
+        o_sb = [keep.tile([128, 4096], F32, name="o_sb%d" % h) for h in range(2)]
+        first_c = keep.tile([128, 128], U32, name="first_c", align_bytes=64)
+        first_s = keep.tile([128, 128], U8, name="first_s", align_bytes=64)
         bias0 = keep.tile([128, 4], F32, name="bias0")
         bias1 = keep.tile([128, 512], F32, name="bias1")
+        rolled = keep.tile([128, 512], BF16, name="rolled")
 
-        def regroup(dst, src, copy=nc.vector.tensor_copy):
-            copy(
+        def regroup(dst, src):
+            nc.vector.tensor_copy(
                 out=dst.rearrange("p (c i t) -> p c t i", i=4, t=4),
                 in_=src.rearrange("p t (c i) -> p c t i", i=4),
             )
@@ -105,38 +120,35 @@ def tile_capsuleneuralnetwork_pa_kernel(tc, primary_input, prev, col, W0, b0, W1
         accs = {}
         ys = {}
 
-        def transpose_inputs(t, passes=range(PASSES)):
+        def transpose_inputs(u, passes=range(PASSES)):
             for g in passes:
-                words = (prim[t] if g < 2 else prv[t])[:].bitcast(F32)
-                base = 256 * g if g < 2 else 0
+                words = (prim[u] if g < 2 else prv[u])[:].bitcast(F32)
                 bank = ps_t.tile([128, 2, 2, 128], F32, name="bank", tag="tp")
-                banks[(t, g)] = bank
-                for half in range(2):
+                banks[(u, g)] = bank
+                for i in range(2):
+                    base = 512 * i + 256 * g if g < 2 else 256 * i
                     for e in range(2):
-                        nc.tensor.transpose(bank[:, half, e, :], words[:, half, base + e:base + 256:2], ident[:])
+                        nc.tensor.transpose(bank[:, i, e, :], words[:, base + e:base + 256:2], ident[:])
 
-        def copy_inputs(t, passes=range(PASSES)):
+        def copy_inputs(u, passes=range(PASSES)):
             if 0 in passes:
                 both = stage.tile([128, 2048], BF16, name="x_g01", tag="x_g01", align_bytes=64)
                 last = stage.tile([128, 1024], BF16, name="x_g2", tag="x_g2", align_bytes=64)
-                x_g[t] = (both, last)
-            both, last = x_g[t]
+                x_g[u] = (both, last)
+            both, last = x_g[u]
             for g in passes:
                 grp = both[:, 1024 * g:1024 * g + 1024] if g < 2 else last[:]
-                dst = grp.bitcast(F32).rearrange("p (t b h) -> p t b h", t=2, b=128, h=2)
-                src = banks[(t, g)][:].rearrange("p t h b -> p t b h")
-                nc.scalar.copy(out=dst, in_=src)
+                dst = grp.bitcast(F32).rearrange("p (i b e) -> p i b e", i=2, b=128, e=2)
+                nc.scalar.copy(out=dst, in_=banks[(u, g)][:].rearrange("p i e b -> p i b e"))
 
-        def quantise_inputs(t, passes):
-            both, last = x_g[t]
+        def quantise_inputs(u, passes):
+            both, last = x_g[u]
             if passes == (0, 1):
-                quantise(x_c[t][:, 0:2, :].rearrange("p g n -> p (g n)"),
-                         x_s[t][:, 0:2, :].rearrange("p g n -> p (g n)"), both[:])
-            elif passes == (2,):
-                quantise(x_c[t][:, 2, :], x_s[t][:, 2, :], last[:])
+                quantise(x_c[u][:, 0:2, :].rearrange("p g n -> p (g n)"),
+                         x_s[u][:, 0:2, :].rearrange("p g n -> p (g n)"), both[:])
             else:
                 (g,) = passes
-                quantise(x_c[t][:, g, :], x_s[t][:, g, :], both[:, 1024 * g:1024 * g + 1024])
+                quantise(x_c[u][:, g, :], x_s[u][:, g, :], both[:, 1024 * g:1024 * g + 1024] if g < 2 else last[:])
 
         def regroup_weights(g):
             if g == 3:
@@ -154,7 +166,12 @@ def tile_capsuleneuralnetwork_pa_kernel(tc, primary_input, prev, col, W0, b0, W1
         def quantise_weights(g):
             quantise(w_c[g][:], w_s[g][:], w_g[g][:])
 
-        rolled = keep.tile([128, 512], BF16, name="rolled")
+        def part_weights():
+            for (dst_c, dst_s, parts) in ((own_c, own_s, ((0, 64), (64, 96))), (next_c, next_s, ((96, 128),))):
+                for (p0, p1) in parts:
+                    nc.sync.dma_start(out=dst_c[p0:p1, :].bitcast(I32), in_=w_c[3][p0:p1, :].bitcast(I32))
+                    for p in range(p0, p1, 32):
+                        nc.sync.dma_start(out=dst_s[p:p + 4, :].bitcast(I32), in_=w_s[3][p:p + 4, :].bitcast(I32))
 
         def roll_bias_rows():
             dst = rolled[:].rearrange("p (j c i) -> p j c i", j=4, i=4)
@@ -172,116 +189,136 @@ def tile_capsuleneuralnetwork_pa_kernel(tc, primary_input, prev, col, W0, b0, W1
             nc.tensor.matmul(out=pb1[:], lhsT=col_ones[:], rhs=bias_rows[:, 512:1024], start=True, stop=True)
             nc.scalar.copy(out=bias1[:], in_=pb1[:])
 
-        def layer1(t):
-            for pair in range(2):
-                acc = ps_a.tile([128, 2, 256], F32, name="acc", tag="acc")
-                accs[(t, pair)] = acc
-                for i in range(2):
-                    j = 2 * pair + i
-                    for g in range(PASSES):
-                        nc.tensor.matmul_mx(
-                            out=acc[:, i, :],
-                            lhsT=w_c[g][:, 128 * j:128 * j + 128].bitcast(FP8X4),
-                            lhsT_scale=w_s[g][:, 128 * j:128 * j + 128],
-                            rhs=x_c[t][:, g, :].bitcast(FP8X4),
-                            rhs_scale=x_s[t][:, g, :],
-                            start=(g == 0),
-                            stop=(g == PASSES - 1),
-                        )
+        def layer1_pass(dst, u, j, g, cols):
+            nc.tensor.matmul_mx(
+                out=dst,
+                lhsT=w_c[g][:, 128 * j:128 * j + 128].bitcast(FP8X4),
+                lhsT_scale=w_s[g][:, 128 * j:128 * j + 128],
+                rhs=x_c[u][:, g, cols].bitcast(FP8X4),
+                rhs_scale=x_s[u][:, g, cols],
+                start=(g == 0),
+                stop=(g == PASSES - 1),
+            )
 
         def layer1_first(g):
             for j in range(4):
                 if g == 0:
                     pool, tag = (ps_a, "acc") if j < 3 else (ps_y, "y")
                     first = pool.tile([128, 512], F32, name="first", tag=tag)
-                    accs[(0, j)] = first
-                nc.tensor.matmul_mx(
-                    out=accs[(0, j)][:, 0:256],
-                    lhsT=w_c[g][:, 128 * j:128 * j + 128].bitcast(FP8X4),
-                    lhsT_scale=w_s[g][:, 128 * j:128 * j + 128],
-                    rhs=x_c[0][:, g, :].bitcast(FP8X4),
-                    rhs_scale=x_s[0][:, g, :],
-                    start=(g == 0),
-                    stop=(g == PASSES - 1),
-                )
+                    accs[(0, j)] = first[:, 0:256]
+                layer1_pass(accs[(0, j)], 0, j, g, slice(0, 256))
 
-        def relu_h(t):
+        def layer1(u):
+            for pair in range(2):
+                acc = ps_a.tile([128, 2, 256], F32, name="acc", tag="acc")
+                for i in range(2):
+                    accs[(u, 2 * pair + i)] = acc[:, i, :]
+                    for g in range(PASSES):
+                        layer1_pass(acc[:, i, :], u, 2 * pair + i, g, slice(0, 256))
+
+        def layer1_row(u, i):
+            acc = ps_a.tile([128, 4, 128], F32, name="acc_row", tag="acc")
             for j in range(4):
-                src = accs[(t, j)][:, 0:256] if t == 0 else accs[(t, j // 2)][:, j % 2, :]
-                nc.scalar.activation(out=h_t[t][:, j, :], in_=src, func=RELU, bias=bias0[:, j:j + 1], scale=1.0)
-
-        def regroup_h(t, copy=nc.vector.tensor_copy):
-            regroup(h_g[t][:], h_t[t][:], copy)
-
-        def roll_h(t, copy=nc.vector.tensor_copy):
-            copy(out=h_g[(t - 1) % UNITS][96:128, :], in_=h_g[t][96:128, :])
-
-        def layer1_half(t, half):
-            acc = ps_a.tile([128, 4, 128], F32, name="acc_half", tag="acc")
-            accs[(t, half)] = acc
-            cols = slice(128 * half, 128 * half + 128)
-            for j in range(4):
+                accs[(u, j, i)] = acc[:, j, :]
                 for g in range(PASSES):
-                    nc.tensor.matmul_mx(
-                        out=acc[:, j, :],
-                        lhsT=w_c[g][:, 128 * j:128 * j + 128].bitcast(FP8X4),
-                        lhsT_scale=w_s[g][:, 128 * j:128 * j + 128],
-                        rhs=x_c[t][:, g, cols].bitcast(FP8X4),
-                        rhs_scale=x_s[t][:, g, cols],
-                        start=(g == 0),
-                        stop=(g == PASSES - 1),
-                    )
+                    layer1_pass(acc[:, j, :], u, j, g, slice(128 * i, 128 * i + 128))
 
-        def relu_h_half(t, half):
-            cols = slice(128 * half, 128 * half + 128)
+        def relu_h(u):
             for j in range(4):
-                nc.scalar.activation(out=h_t[t][:, j, cols], in_=accs[(t, half)][:, j, :], func=RELU,
+                nc.scalar.activation(out=h_t[u][:, j, :], in_=accs[(u, j)], func=RELU, bias=bias0[:, j:j + 1], scale=1.0)
+
+        def relu_h_row(u, i):
+            for j in range(4):
+                nc.scalar.activation(out=h_t[u][:, j, 128 * i:128 * i + 128], in_=accs[(u, j, i)], func=RELU,
                                      bias=bias0[:, j:j + 1], scale=1.0)
 
-        def regroup_and_roll_last_h(half, copy=nc.vector.tensor_copy):
-            cols, words = slice(128 * half, 128 * half + 128), slice(512 * half, 512 * half + 512)
-            regroup(h_g[UNITS - 2][96:128, words], h_t[UNITS - 1][96:128, :, cols])
-            regroup(h_g[UNITS - 1][0:96, words], h_t[UNITS - 1][0:96, :, cols], copy)
-
-        def quantise_h(t):
-            quantise(h_c[t][:], h_s[t][:], h_g[t][:])
-
-        def quantise_h_half(t, half):
-            cols = slice(128 * half, 128 * half + 128)
-            quantise(h_c[t][:, cols], h_s[t][:, cols], h_g[t][:, 512 * half:512 * half + 512])
-
-        def store(t, half):
-            rows = out[128 * half:128 * half + 128, :]
-            if t < UNITS - 1:
-                nc.sync.dma_start(out=rows[:, 512 * t + 128:512 * t + 640], in_=o_sb[t][:, half, :])
+        def regroup_h(u):
+            half, v = divmod(u, 4)
+            if v < 3:
+                regroup(h_g[half][:, 1024 * v:1024 * v + 1024], h_t[u][:])
             else:
-                nc.sync.dma_start(out=rows[:, 3712:4096], in_=o_sb[t][:, half, 0:384])
-                nc.sync.dma_start(out=rows[:, 0:128], in_=o_sb[t][:, half, 384:512])
+                regroup(h_g[half][96:128, 2560:3584], h_t[u][96:128])
+                regroup(h_g[half][0:96, 3072:4096], h_t[u][0:96])
 
-        def layer2(t, halves=(0, 1), pool=ps_y, tag="y"):
-            for half in halves:
+        def roll_h(u):
+            half, v = divmod(u, 4)
+            for t in (2 * v, 2 * v + 1):
+                if v < 3 and (half, t) != (1, 0):
+                    to = 512 * ((t - 1) % 8)
+                    nc.vector.tensor_copy(out=h_g[half][96:128, to:to + 512], in_=h_g[half][96:128, 512 * t:512 * t + 512])
+
+        def regroup_row(u, i):
+            half, v = divmod(u, 4)
+            t = 2 * v + i
+            regroup(h_g[half][:, 512 * t:512 * t + 512], h_t[u][:, :, 128 * i:128 * i + 128])
+
+        def quantise_h(half, t0, t1):
+            quantise(h_c[half][:, 128 * t0:128 * t1], h_s[half][:, 128 * t0:128 * t1], h_g[half][:, 512 * t0:512 * t1])
+
+        def layer2(half, t, pool=ps_y, tag="y"):
+            y = pool.tile([128, 512], F32, name="y", tag=tag)
+            ys[(half, t)] = y
+            nc.tensor.matmul_mx(
+                out=y[:],
+                lhsT=h_c[half][:, 128 * t:128 * t + 128].bitcast(FP8X4),
+                lhsT_scale=h_s[half][:, 128 * t:128 * t + 128],
+                rhs=w_c[3][:].bitcast(FP8X4),
+                rhs_scale=w_s[3][:],
+                start=True,
+                stop=True,
+            )
+
+        def layer2_part(half, t, part, start, pool=ps_y, tag="y"):
+            if start:
                 y = pool.tile([128, 512], F32, name="y", tag=tag)
-                ys[(t, half)] = y
-                nc.tensor.matmul_mx(
-                    out=y[:],
-                    lhsT=h_c[t][:, 128 * half:128 * half + 128].bitcast(FP8X4),
-                    lhsT_scale=h_s[t][:, 128 * half:128 * half + 128],
-                    rhs=w_c[3][:].bitcast(FP8X4),
-                    rhs_scale=w_s[3][:],
-                    start=True,
-                    stop=True,
-                )
+                ys[(half, t)] = y
+            if part == "own":
+                cols = slice(128 * t, 128 * t + 128)
+                codes, scales, w1_c, w1_s = h_c[half][:, cols], h_s[half][:, cols], own_c, own_s
+            elif t < 7:
+                cols = slice(128 * t + 128, 128 * t + 256)
+                codes, scales, w1_c, w1_s = h_c[half][:, cols], h_s[half][:, cols], next_c, next_s
+            else:
+                codes, scales, w1_c, w1_s = first_c[:], first_s[:], next_c, next_s
+            nc.tensor.matmul_mx(
+                out=ys[(half, t)][:],
+                lhsT=codes.bitcast(FP8X4),
+                lhsT_scale=scales,
+                rhs=w1_c[:].bitcast(FP8X4),
+                rhs_scale=w1_s[:],
+                start=start,
+                stop=not start,
+            )
 
-        def add_bias(t, half):
-            nc.vector.tensor_tensor(out=o_sb[t][:, half, :], in0=ys[(t, half)][:], in1=bias1[:], op=ADD)
+        def add_bias(half, t, a=0, b=512):
+            nc.vector.tensor_tensor(out=o_sb[half][:, 512 * t + a:512 * t + b], in0=ys[(half, t)][:, a:b],
+                                    in1=bias1[:, a:b], op=ADD)
 
-        def finish(t, half, engine):
-            piece = o_sb[t][:, half, :]
+        def last_relu(half, t, engine, a=0, b=512):
+            piece = o_sb[half][:, 512 * t + a:512 * t + b]
             if engine is nc.scalar:
                 nc.scalar.activation(out=piece, in_=piece, func=RELU)
             else:
                 nc.vector.tensor_scalar_max(piece, piece, 0.0)
-            store(t, half)
+
+        def store(half, t0, t1):
+            rows = out[128 * half:128 * half + 128, :]
+            c0, c1 = 512 * t0 + 128, min(512 * t1 + 128, 4096)
+            nc.sync.dma_start(out=rows[:, c0:c1], in_=o_sb[half][:, c0 - 128:c1 - 128])
+            if t1 == 8:
+                nc.sync.dma_start(out=rows[:, 0:128], in_=o_sb[half][:, 3968:4096])
+
+        def rows_of(u):
+            half, v = divmod(u, 4)
+            return ((half, 2 * v), (half, 2 * v + 1))
+
+        def quantise_rows(u):
+            half, v = divmod(u, 4)
+            quantise_h(half, 2 * v, 2 * v + 2)
+
+        def store_rows(u):
+            half, v = divmod(u, 4)
+            store(half, 2 * v, 2 * v + 2)
 
         transpose_inputs(0)
         copy_inputs(0, (0, 1))
@@ -299,15 +336,11 @@ def tile_capsuleneuralnetwork_pa_kernel(tc, primary_input, prev, col, W0, b0, W1
         regroup_weights(2)
         quantise_inputs(0, (2,))
         quantise_weights(2)
-        regroup_weights(3)
         transpose_inputs(1, (0, 1))
         copy_inputs(1, (0, 1))
         layer1_first(2)
         transpose_inputs(1, (2,))
         copy_inputs(1, (2,))
-        quantise_inputs(1, (0, 1))
-        quantise_weights(3)
-        quantise_inputs(1, (2,))
 
         for s in range(UNITS - 2):
             if s > 0:
@@ -315,71 +348,89 @@ def tile_capsuleneuralnetwork_pa_kernel(tc, primary_input, prev, col, W0, b0, W1
             relu_h(s)
             if s + 2 < UNITS:
                 transpose_inputs(s + 2, (0,))
+            if s == 5:
+                quantise(first_c[:], first_s[:], h_g[1][:, 0:512])
             if s >= 1:
                 roll_h(s - 1)
             if s >= 3:
-                finish(s - 3, 0, nc.vector)
-                finish(s - 3, 1, nc.scalar)
+                last_relu(*rows_of(s - 3)[0], nc.scalar)
+                last_relu(*rows_of(s - 3)[1], nc.scalar)
+                store_rows(s - 3)
             if s >= 2:
-                quantise_h(s - 2)
-            if s > 0:
-                quantise_inputs(s + 1, (0, 1))
-            if s > 0:
-                quantise_inputs(s + 1, (2,))
+                quantise_rows(s - 2)
+            quantise_inputs(s + 1, (0, 1))
+            quantise_inputs(s + 1, (2,))
+            if s == 0:
+                regroup_weights(3)
+            if s == 1:
+                quantise_weights(3)
             if s >= 2:
-                layer2(s - 2)
+                for row in rows_of(s - 2):
+                    layer2(*row)
             if s + 2 < UNITS:
                 transpose_inputs(s + 2, (1, 2))
                 copy_inputs(s + 2)
+            if s == 3:
+                part_weights()
             regroup_h(s)
             if s >= 2:
-                add_bias(s - 2, 0)
-            if s >= 2:
-                add_bias(s - 2, 1)
+                for row in rows_of(s - 2):
+                    add_bias(*row)
 
         layer1(6)
         relu_h(6)
         roll_h(5)
-        finish(3, 0, nc.vector)
-        quantise_h(4)
+        last_relu(*rows_of(3)[0], nc.scalar)
+        last_relu(*rows_of(3)[1], nc.scalar)
+        store_rows(3)
+        quantise_rows(4)
         quantise_inputs(7, (0, 1))
         quantise_inputs(7, (2,))
-        layer2(4)
-        layer1_half(7, 0)
-        layer1_half(7, 1)
+        quantise_rows(5)
+        for row in rows_of(4):
+            layer2(*row)
+        layer1_row(7, 0)
+        layer2(1, 2, ps_t, "tp")
+        layer2_part(1, 3, "own", True, ps_t, "tp")
+        layer1_row(7, 1)
+        relu_h_row(7, 0)
+        relu_h_row(7, 1)
+        add_bias(1, 0)
         regroup_h(6)
-        add_bias(4, 0)
-        roll_h(6)
-        relu_h_half(7, 0)
-        relu_h_half(7, 1)
-        add_bias(4, 1)
-        quantise_h(5)
-        layer2(5)
-        regroup_and_roll_last_h(0)
-        finish(3, 1, nc.scalar)
-        add_bias(5, 0)
-        quantise_h_half(6, 0)
-        quantise_h_half(7, 0)
-        layer2(6, (0,), ps_t, "tp")
-        layer2(7, (0,), ps_t, "tp")
-        regroup_and_roll_last_h(1)
-        finish(4, 0, nc.scalar)
-        finish(4, 1, nc.scalar)
-        add_bias(5, 1)
-        quantise_h_half(6, 1)
-        quantise_h_half(7, 1)
-        layer2(6, (1,), ps_t, "tp")
-        layer2(7, (1,))
-        finish(5, 0, nc.scalar)
-        finish(5, 1, nc.scalar)
-        for (t, half) in ((6, 0), (7, 0), (6, 1)):
-            add_bias(t, half)
-            finish(t, half, nc.scalar)
-        for (a, b, engine) in ((0, 256, nc.scalar), (256, 512, nc.vector)):
-            piece = o_sb[7][:, 1, a:b]
-            nc.vector.tensor_tensor(out=piece, in0=ys[(7, 1)][:, a:b], in1=bias1[:, a:b], op=ADD)
-            if engine is nc.scalar:
-                nc.scalar.activation(out=piece, in_=piece, func=RELU)
-            else:
-                nc.vector.tensor_scalar_max(piece, piece, 0.0)
-        store(7, 1)
+        add_bias(1, 1)
+        quantise_h(1, 4, 6)
+        last_relu(1, 0, nc.scalar)
+        last_relu(1, 1, nc.scalar)
+        store(1, 0, 2)
+        layer2_part(1, 3, "next", False)
+        layer2_part(1, 4, "own", True)
+        layer2_part(1, 4, "next", False)
+        layer2_part(1, 5, "own", True)
+        regroup_row(7, 0)
+        add_bias(1, 2)
+        quantise_h(1, 6, 7)
+        last_relu(1, 2, nc.scalar)
+        layer2_part(1, 5, "next", False)
+        layer2_part(1, 6, "own", True, ps_t, "tp")
+        add_bias(1, 3)
+        regroup_row(7, 1)
+        add_bias(1, 4)
+        quantise_h(1, 7, 8)
+        last_relu(1, 3, nc.scalar)
+        store(1, 2, 4)
+        layer2_part(1, 7, "next", True, ps_t, "tp")
+        layer2_part(1, 6, "next", False)
+        layer2_part(1, 7, "own", False)
+        last_relu(1, 4, nc.scalar)
+        store(1, 4, 5)
+        add_bias(1, 5)
+        last_relu(1, 5, nc.scalar)
+        store(1, 5, 6)
+        add_bias(1, 6)
+        last_relu(1, 6, nc.scalar)
+        store(1, 6, 7)
+        add_bias(1, 7, 0, 256)
+        last_relu(1, 7, nc.scalar, 0, 256)
+        add_bias(1, 7, 256, 512)
+        last_relu(1, 7, nc.vector, 256, 512)
+        store(1, 7, 8)

@@ -80,8 +80,8 @@ def tile_capsuleneuralnetwork_pa_kernel(tc, primary_input, prev, col, W0, b0, W1
         load_w0(0)
         load_prev(0)
         load_w0(1)
-        load_w0(2)
         load_primary(1)
+        load_w0(2)
         load_prev(1)
         load_primary(2)
         load_prev(2)
@@ -160,8 +160,8 @@ def tile_capsuleneuralnetwork_pa_kernel(tc, primary_input, prev, col, W0, b0, W1
                 if g < 2:
                     nc.vector.tensor_copy(out=dst[:, :, c0:c1], in_=src[:, :, r0:r0 + c1 - c0])
                 else:
-                    nc.vector.tensor_copy(out=dst[:, 0:2, c0:c1], in_=src[:, 0:2, r0:r0 + c1 - c0])
-                    nc.scalar.copy(out=dst[:, 2:4, c0:c1], in_=src[:, 2:4, r0:r0 + c1 - c0])
+                    nc.vector.tensor_copy(out=dst[:, 0:3, c0:c1], in_=src[:, 0:3, r0:r0 + c1 - c0])
+                    nc.scalar.copy(out=dst[:, 3:4, c0:c1], in_=src[:, 3:4, r0:r0 + c1 - c0])
 
         def quantise_weights(g):
             quantise(w_c[g][:], w_s[g][:], w_g[g][:])
@@ -329,31 +329,33 @@ def tile_capsuleneuralnetwork_pa_kernel(tc, primary_input, prev, col, W0, b0, W1
         quantise_inputs(0, (0,))
         quantise_weights(0)
         layer1_first(0)
+        transpose_inputs(1, (0, 1))
+        copy_inputs(1, (0,))
         regroup_weights(1)
         quantise_inputs(0, (1,))
         quantise_weights(1)
         layer1_first(1)
         regroup_weights(2)
+        copy_inputs(1, (1,))
         quantise_inputs(0, (2,))
         quantise_weights(2)
-        transpose_inputs(1, (0, 1))
-        copy_inputs(1, (0, 1))
-        layer1_first(2)
         transpose_inputs(1, (2,))
         copy_inputs(1, (2,))
+        transpose_inputs(2, (0,))
+        layer1_first(2)
 
         for s in range(UNITS - 2):
             if s > 0:
                 layer1(s)
             relu_h(s)
-            if s + 2 < UNITS:
+            if 0 < s < UNITS - 2:
                 transpose_inputs(s + 2, (0,))
             if s == 5:
                 quantise(first_c[:], first_s[:], h_g[1][:, 0:512])
             if s >= 1:
                 roll_h(s - 1)
             if s >= 3:
-                last_relu(*rows_of(s - 3)[0], nc.scalar)
+                last_relu(*rows_of(s - 3)[0], nc.vector)
                 last_relu(*rows_of(s - 3)[1], nc.scalar)
                 store_rows(s - 3)
             if s >= 2:

from contextlib import ExitStack

import concourse.mybir as mybir
from concourse.masks import make_identity

F32 = mybir.dt.float32
BF16 = mybir.dt.bfloat16
U32 = mybir.dt.uint32
U8 = mybir.dt.uint8
I32 = mybir.dt.int32
FP8X4 = mybir.dt.float8_e4m3fn_x4
RELU = mybir.ActivationFunctionType.Relu
ADD = mybir.AluOpType.add

FLOPS = 2 * 2048 * (1536 * 512 + 512 * 512)

UNITS = 8
PASSES = 3


def tile_capsuleneuralnetwork_pa_kernel(tc, primary_input, prev, col, W0, b0, W1, b1, out):
    nc = tc.nc
    with ExitStack() as ctx:
        keep = ctx.enter_context(tc.tile_pool(name="keep", bufs=1))
        stage = ctx.enter_context(tc.tile_pool(name="stage", bufs=2))
        ps_t = ctx.enter_context(tc.psum_pool(name="ps_t", bufs=3))
        ps_a = ctx.enter_context(tc.psum_pool(name="ps_a", bufs=3))
        ps_y = ctx.enter_context(tc.psum_pool(name="ps_y", bufs=2))
        ctx.enter_context(tc.manual_schedule())

        ident = keep.tile([128, 128], F32, name="ident")
        make_identity(nc, ident[:])
        bias_rows = keep.tile([128, 1024], BF16, name="bias_rows")
        nc.vector.memset(bias_rows[:], 0.0)
        col_ones = keep.tile([128, 128], BF16, name="col_ones")
        nc.gpsimd.memset(col_ones[:], 0.0)
        nc.gpsimd.memset(col_ones[32:64, :], 1.0)
        col_sb = keep.tile([1, 1], BF16, name="col_sb")
        nc.scalar.dma_start(out=col_sb[0:1, 0:1], in_=col.unsqueeze(0))
        nc.gpsimd.tensor_copy(out=col_ones[0:1, :], in_=col_sb[0:1, 0:1].to_broadcast([1, 128]))
        nc.scalar.dma_start(out=bias_rows[0:1, 0:512], in_=W0[1536:1537, :])
        nc.scalar.dma_start(out=bias_rows[32:33, 0:512], in_=b0.unsqueeze(0))
        nc.scalar.dma_start(out=bias_rows[0:1, 512:1024], in_=W1[512:513, :])
        nc.scalar.dma_start(out=bias_rows[32:33, 512:1024], in_=b1.unsqueeze(0))
        warm = keep.tile([128, 1], F32, name="warm")
        nc.gpsimd.memset(warm[:], 0.0)
        nc.scalar.activation(out=warm[:], in_=warm[:], func=RELU)

        own_c = keep.tile([128, 512], U32, name="own_c", align_bytes=64)
        own_s = keep.tile([128, 512], U8, name="own_s", align_bytes=64)
        next_c = keep.tile([128, 512], U32, name="next_c", align_bytes=64)
        next_s = keep.tile([128, 512], U8, name="next_s", align_bytes=64)
        nc.gpsimd.memset(own_c[96:128, :], 0)
        nc.gpsimd.memset(next_c[0:96, :], 0)
        nc.gpsimd.memset(own_s[:].bitcast(U32), 0)
        nc.gpsimd.memset(next_s[:].bitcast(U32), 0)

        prim = [keep.tile([128, 2048], BF16, name="prim%d" % u) for u in range(UNITS)]
        prv = [keep.tile([128, 1024], BF16, name="prv%d" % u) for u in range(UNITS)]
        w_raw = [keep.tile([128, 4, 512], BF16, name="w_raw%d" % g) for g in range(4)]

        def load_primary(u):
            half, v = divmod(u, 4)
            nc.sync.dma_start(out=prim[u][:],
                              in_=primary_input[128 * half:128 * half + 128, 2048 * v:2048 * v + 2048])

        def load_prev(u):
            half, v = divmod(u, 4)
            nc.sync.dma_start(out=prv[u][:], in_=prev[128 * half:128 * half + 128, 1024 * v:1024 * v + 1024])

        def load_w0(g):
            nc.sync.dma_start(out=w_raw[g][:], in_=W0[512 * g:512 * g + 512, :].rearrange("(p j) c -> p j c", j=4))

        def load_w1():
            rows = W1[0:512, :].rearrange("(c j i) n -> j c i n", j=4, i=4)
            for j in range(4):
                nc.sync.dma_start(out=w_raw[3][:, j, :], in_=rows[j])

        load_primary(0)
        load_w0(0)
        load_prev(0)
        load_w0(1)
        load_primary(1)
        load_w0(2)
        load_prev(1)
        load_primary(2)
        load_prev(2)
        load_w1()
        for u in range(3, UNITS):
            load_primary(u)
            load_prev(u)

        w_g = [keep.tile([128, 2048], BF16, name="w_g%d" % g, align_bytes=64) for g in range(4)]
        w_c = [keep.tile([128, 512], U32, name="w_c%d" % g, align_bytes=64) for g in range(4)]
        w_s = [keep.tile([128, 512], U8, name="w_s%d" % g, align_bytes=64) for g in range(4)]
        x_c = [keep.tile([128, PASSES, 256], U32, name="x_c%d" % u, align_bytes=64) for u in range(UNITS)]
        x_s = [keep.tile([128, PASSES, 256], U8, name="x_s%d" % u, align_bytes=64) for u in range(UNITS)]
        h_t = [keep.tile([128, 4, 256], BF16, name="h_t%d" % u) for u in range(UNITS)]
        h_g = [keep.tile([128, 4096], BF16, name="h_g%d" % h, align_bytes=64) for h in range(2)]
        h_c = [keep.tile([128, 1024], U32, name="h_c%d" % h, align_bytes=64) for h in range(2)]
        h_s = [keep.tile([128, 1024], U8, name="h_s%d" % h, align_bytes=64) for h in range(2)]
        o_sb = [keep.tile([128, 4096], F32, name="o_sb%d" % h) for h in range(2)]
        first_c = keep.tile([128, 128], U32, name="first_c", align_bytes=64)
        first_s = keep.tile([128, 128], U8, name="first_s", align_bytes=64)
        bias0 = keep.tile([128, 4], F32, name="bias0")
        bias1 = keep.tile([128, 512], F32, name="bias1")
        rolled = keep.tile([128, 512], BF16, name="rolled")

        def regroup(dst, src):
            nc.vector.tensor_copy(
                out=dst.rearrange("p (c i t) -> p c t i", i=4, t=4),
                in_=src.rearrange("p t (c i) -> p c t i", i=4),
            )

        def quantise(codes, scales, src):
            nc.vector.quantize_mx(out=codes.bitcast(FP8X4), scales=scales, in_=src)

        banks = {}
        x_g = {}
        accs = {}
        ys = {}

        def transpose_inputs(u, passes=range(PASSES)):
            for g in passes:
                words = (prim[u] if g < 2 else prv[u])[:].bitcast(F32)
                bank = ps_t.tile([128, 2, 2, 128], F32, name="bank", tag="tp")
                banks[(u, g)] = bank
                for i in range(2):
                    base = 512 * i + 256 * g if g < 2 else 256 * i
                    for e in range(2):
                        nc.tensor.transpose(bank[:, i, e, :], words[:, base + e:base + 256:2], ident[:])

        def copy_inputs(u, passes=range(PASSES)):
            if 0 in passes:
                both = stage.tile([128, 2048], BF16, name="x_g01", tag="x_g01", align_bytes=64)
                last = stage.tile([128, 1024], BF16, name="x_g2", tag="x_g2", align_bytes=64)
                x_g[u] = (both, last)
            both, last = x_g[u]
            for g in passes:
                grp = both[:, 1024 * g:1024 * g + 1024] if g < 2 else last[:]
                dst = grp.bitcast(F32).rearrange("p (i b e) -> p i b e", i=2, b=128, e=2)
                nc.scalar.copy(out=dst, in_=banks[(u, g)][:].rearrange("p i e b -> p i b e"))

        def quantise_inputs(u, passes):
            both, last = x_g[u]
            if passes == (0, 1):
                quantise(x_c[u][:, 0:2, :].rearrange("p g n -> p (g n)"),
                         x_s[u][:, 0:2, :].rearrange("p g n -> p (g n)"), both[:])
            else:
                (g,) = passes
                quantise(x_c[u][:, g, :], x_s[u][:, g, :], both[:, 1024 * g:1024 * g + 1024] if g < 2 else last[:])

        def regroup_weights(g):
            if g == 3:
                regroup(w_g[g][:], w_raw[g][:])
                return
            dst = w_g[g][:].rearrange("p (t c i j) -> p t c j i", t=4, c=32, i=4, j=4)
            src = w_raw[g][:].rearrange("p j (c t i) -> p t c j i", c=32, t=4, i=4)
            for (c0, c1, r0) in ((0, 24, 8), (24, 32, 0)):
                if g < 2:
                    nc.vector.tensor_copy(out=dst[:, :, c0:c1], in_=src[:, :, r0:r0 + c1 - c0])
                else:
                    nc.vector.tensor_copy(out=dst[:, 0:3, c0:c1], in_=src[:, 0:3, r0:r0 + c1 - c0])
                    nc.scalar.copy(out=dst[:, 3:4, c0:c1], in_=src[:, 3:4, r0:r0 + c1 - c0])

        def quantise_weights(g):
            quantise(w_c[g][:], w_s[g][:], w_g[g][:])

        def part_weights():
            for (dst_c, dst_s, parts) in ((own_c, own_s, ((0, 64), (64, 96))), (next_c, next_s, ((96, 128),))):
                for (p0, p1) in parts:
                    nc.sync.dma_start(out=dst_c[p0:p1, :].bitcast(I32), in_=w_c[3][p0:p1, :].bitcast(I32))
                    for p in range(p0, p1, 32):
                        nc.sync.dma_start(out=dst_s[p:p + 4, :].bitcast(I32), in_=w_s[3][p:p + 4, :].bitcast(I32))

        def roll_bias_rows():
            dst = rolled[:].rearrange("p (j c i) -> p j c i", j=4, i=4)
            src = bias_rows[:, 0:512].rearrange("p (c j i) -> p j c i", j=4, i=4)
            nc.scalar.copy(out=dst[:, :, 0:24, :], in_=src[:, :, 8:32, :])
            nc.scalar.copy(out=dst[:, :, 24:32, :], in_=src[:, :, 0:8, :])

        def biases():
            pb0 = ps_t.tile([128, 4, 64], F32, name="pb0", tag="tp")
            for j in range(4):
                nc.tensor.matmul(out=pb0[:, j, :], lhsT=rolled[:, 128 * j:128 * j + 128], rhs=col_ones[:, 0:64],
                                 start=True, stop=True)
            nc.scalar.copy(out=bias0[:], in_=pb0[:, :, 0])
            pb1 = ps_t.tile([128, 512], F32, name="pb1", tag="tp")
            nc.tensor.matmul(out=pb1[:], lhsT=col_ones[:], rhs=bias_rows[:, 512:1024], start=True, stop=True)
            nc.scalar.copy(out=bias1[:], in_=pb1[:])

        def layer1_pass(dst, u, j, g, cols):
            nc.tensor.matmul_mx(
                out=dst,
                lhsT=w_c[g][:, 128 * j:128 * j + 128].bitcast(FP8X4),
                lhsT_scale=w_s[g][:, 128 * j:128 * j + 128],
                rhs=x_c[u][:, g, cols].bitcast(FP8X4),
                rhs_scale=x_s[u][:, g, cols],
                start=(g == 0),
                stop=(g == PASSES - 1),
            )

        def layer1_first(g):
            for j in range(4):
                if g == 0:
                    pool, tag = (ps_a, "acc") if j < 3 else (ps_y, "y")
                    first = pool.tile([128, 512], F32, name="first", tag=tag)
                    accs[(0, j)] = first[:, 0:256]
                layer1_pass(accs[(0, j)], 0, j, g, slice(0, 256))

        def layer1(u):
            for pair in range(2):
                acc = ps_a.tile([128, 2, 256], F32, name="acc", tag="acc")
                for i in range(2):
                    accs[(u, 2 * pair + i)] = acc[:, i, :]
                    for g in range(PASSES):
                        layer1_pass(acc[:, i, :], u, 2 * pair + i, g, slice(0, 256))

        def layer1_row(u, i):
            acc = ps_a.tile([128, 4, 128], F32, name="acc_row", tag="acc")
            for j in range(4):
                accs[(u, j, i)] = acc[:, j, :]
                for g in range(PASSES):
                    layer1_pass(acc[:, j, :], u, j, g, slice(128 * i, 128 * i + 128))

        def relu_h(u):
            for j in range(4):
                nc.scalar.activation(out=h_t[u][:, j, :], in_=accs[(u, j)], func=RELU, bias=bias0[:, j:j + 1], scale=1.0)

        def relu_h_row(u, i):
            for j in range(4):
                nc.scalar.activation(out=h_t[u][:, j, 128 * i:128 * i + 128], in_=accs[(u, j, i)], func=RELU,
                                     bias=bias0[:, j:j + 1], scale=1.0)

        def regroup_h(u):
            half, v = divmod(u, 4)
            if v < 3:
                regroup(h_g[half][:, 1024 * v:1024 * v + 1024], h_t[u][:])
            else:
                regroup(h_g[half][96:128, 2560:3584], h_t[u][96:128])
                regroup(h_g[half][0:96, 3072:4096], h_t[u][0:96])

        def roll_h(u):
            half, v = divmod(u, 4)
            for t in (2 * v, 2 * v + 1):
                if v < 3 and (half, t) != (1, 0):
                    to = 512 * ((t - 1) % 8)
                    nc.vector.tensor_copy(out=h_g[half][96:128, to:to + 512], in_=h_g[half][96:128, 512 * t:512 * t + 512])

        def regroup_row(u, i):
            half, v = divmod(u, 4)
            t = 2 * v + i
            regroup(h_g[half][:, 512 * t:512 * t + 512], h_t[u][:, :, 128 * i:128 * i + 128])

        def quantise_h(half, t0, t1):
            quantise(h_c[half][:, 128 * t0:128 * t1], h_s[half][:, 128 * t0:128 * t1], h_g[half][:, 512 * t0:512 * t1])

        def layer2(half, t, pool=ps_y, tag="y"):
            y = pool.tile([128, 512], F32, name="y", tag=tag)
            ys[(half, t)] = y
            nc.tensor.matmul_mx(
                out=y[:],
                lhsT=h_c[half][:, 128 * t:128 * t + 128].bitcast(FP8X4),
                lhsT_scale=h_s[half][:, 128 * t:128 * t + 128],
                rhs=w_c[3][:].bitcast(FP8X4),
                rhs_scale=w_s[3][:],
                start=True,
                stop=True,
            )

        def layer2_part(half, t, part, start, pool=ps_y, tag="y"):
            if start:
                y = pool.tile([128, 512], F32, name="y", tag=tag)
                ys[(half, t)] = y
            if part == "own":
                cols = slice(128 * t, 128 * t + 128)
                codes, scales, w1_c, w1_s = h_c[half][:, cols], h_s[half][:, cols], own_c, own_s
            elif t < 7:
                cols = slice(128 * t + 128, 128 * t + 256)
                codes, scales, w1_c, w1_s = h_c[half][:, cols], h_s[half][:, cols], next_c, next_s
            else:
                codes, scales, w1_c, w1_s = first_c[:], first_s[:], next_c, next_s
            nc.tensor.matmul_mx(
                out=ys[(half, t)][:],
                lhsT=codes.bitcast(FP8X4),
                lhsT_scale=scales,
                rhs=w1_c[:].bitcast(FP8X4),
                rhs_scale=w1_s[:],
                start=start,
                stop=not start,
            )

        def add_bias(half, t, a=0, b=512):
            nc.vector.tensor_tensor(out=o_sb[half][:, 512 * t + a:512 * t + b], in0=ys[(half, t)][:, a:b],
                                    in1=bias1[:, a:b], op=ADD)

        def last_relu(half, t, engine, a=0, b=512):
            piece = o_sb[half][:, 512 * t + a:512 * t + b]
            if engine is nc.scalar:
                nc.scalar.activation(out=piece, in_=piece, func=RELU)
            else:
                nc.vector.tensor_scalar_max(piece, piece, 0.0)

        def store(half, t0, t1):
            rows = out[128 * half:128 * half + 128, :]
            c0, c1 = 512 * t0 + 128, min(512 * t1 + 128, 4096)
            nc.sync.dma_start(out=rows[:, c0:c1], in_=o_sb[half][:, c0 - 128:c1 - 128])
            if t1 == 8:
                nc.sync.dma_start(out=rows[:, 0:128], in_=o_sb[half][:, 3968:4096])

        def rows_of(u):
            half, v = divmod(u, 4)
            return ((half, 2 * v), (half, 2 * v + 1))

        def quantise_rows(u):
            half, v = divmod(u, 4)
            quantise_h(half, 2 * v, 2 * v + 2)

        def store_rows(u):
            half, v = divmod(u, 4)
            store(half, 2 * v, 2 * v + 2)

        transpose_inputs(0)
        copy_inputs(0, (0, 1))
        roll_bias_rows()
        copy_inputs(0, (2,))
        biases()
        regroup_weights(0)
        quantise_inputs(0, (0,))
        quantise_weights(0)
        layer1_first(0)
        transpose_inputs(1, (0, 1))
        copy_inputs(1, (0,))
        regroup_weights(1)
        quantise_inputs(0, (1,))
        quantise_weights(1)
        layer1_first(1)
        regroup_weights(2)
        copy_inputs(1, (1,))
        quantise_inputs(0, (2,))
        quantise_weights(2)
        transpose_inputs(1, (2,))
        copy_inputs(1, (2,))
        transpose_inputs(2, (0,))
        layer1_first(2)

        for s in range(UNITS - 2):
            if s > 0:
                layer1(s)
            relu_h(s)
            if 0 < s < UNITS - 2:
                transpose_inputs(s + 2, (0,))
            if s == 5:
                quantise(first_c[:], first_s[:], h_g[1][:, 0:512])
            if s >= 1:
                roll_h(s - 1)
            if s >= 3:
                last_relu(*rows_of(s - 3)[0], nc.vector)
                last_relu(*rows_of(s - 3)[1], nc.scalar)
                store_rows(s - 3)
            if s >= 2:
                quantise_rows(s - 2)
            quantise_inputs(s + 1, (0, 1))
            quantise_inputs(s + 1, (2,))
            if s == 0:
                regroup_weights(3)
            if s == 1:
                quantise_weights(3)
            if s >= 2:
                for row in rows_of(s - 2):
                    layer2(*row)
            if s + 2 < UNITS:
                transpose_inputs(s + 2, (1, 2))
                copy_inputs(s + 2)
            if s == 3:
                part_weights()
            regroup_h(s)
            if s >= 2:
                for row in rows_of(s - 2):
                    add_bias(*row)

        layer1(6)
        relu_h(6)
        roll_h(5)
        last_relu(*rows_of(3)[0], nc.scalar)
        last_relu(*rows_of(3)[1], nc.scalar)
        store_rows(3)
        quantise_rows(4)
        quantise_inputs(7, (0, 1))
        quantise_inputs(7, (2,))
        quantise_rows(5)
        for row in rows_of(4):
            layer2(*row)
        layer1_row(7, 0)
        layer2(1, 2, ps_t, "tp")
        layer2_part(1, 3, "own", True, ps_t, "tp")
        layer1_row(7, 1)
        relu_h_row(7, 0)
        relu_h_row(7, 1)
        add_bias(1, 0)
        regroup_h(6)
        add_bias(1, 1)
        quantise_h(1, 4, 6)
        last_relu(1, 0, nc.scalar)
        last_relu(1, 1, nc.scalar)
        store(1, 0, 2)
        layer2_part(1, 3, "next", False)
        layer2_part(1, 4, "own", True)
        layer2_part(1, 4, "next", False)
        layer2_part(1, 5, "own", True)
        regroup_row(7, 0)
        add_bias(1, 2)
        quantise_h(1, 6, 7)
        last_relu(1, 2, nc.scalar)
        layer2_part(1, 5, "next", False)
        layer2_part(1, 6, "own", True, ps_t, "tp")
        add_bias(1, 3)
        regroup_row(7, 1)
        add_bias(1, 4)
        quantise_h(1, 7, 8)
        last_relu(1, 3, nc.scalar)
        store(1, 2, 4)
        layer2_part(1, 7, "next", True, ps_t, "tp")
        layer2_part(1, 6, "next", False)
        layer2_part(1, 7, "own", False)
        last_relu(1, 4, nc.scalar)
        store(1, 4, 5)
        add_bias(1, 5)
        last_relu(1, 5, nc.scalar)
        store(1, 5, 6)
        add_bias(1, 6)
        last_relu(1, 6, nc.scalar)
        store(1, 6, 7)
        add_bias(1, 7, 0, 256)
        last_relu(1, 7, nc.scalar, 0, 256)
        add_bias(1, 7, 256, 512)
        last_relu(1, 7, nc.vector, 256, 512)
        store(1, 7, 8)
